import numpy as np
import ml_dtypes


def mxq(x, axis, fmt="e4m3"):
    dtype, down = {"e4m3": (ml_dtypes.float8_e4m3fn, 7), "e5m2": (ml_dtypes.float8_e5m2, 14)}[fmt]
    v = np.moveaxis(np.asarray(x, np.float32).astype(ml_dtypes.bfloat16).astype(np.float64), axis, -1)
    blocks = v.reshape(v.shape[:-1] + (-1, 32))
    amax = np.abs(blocks).max(-1, keepdims=True)
    byte = np.maximum(np.where(amax > 0, np.frexp(amax)[1] - 1 + 127, 0) - down, 1)
    scale = np.exp2(byte - 127.0)
    codes = (blocks / scale).astype(np.float32).astype(dtype).astype(np.float64)
    return np.moveaxis((codes * scale).reshape(v.shape), -1, axis)


WIDE = False


def mx_kscale(k):
    if not WIDE:
        return np.ones(k)
    levels = np.array([10, -10, 5, -5, 0])
    a = np.random.permutation(np.resize(levels, k // 512 * 4)).reshape(k // 512, 4)
    idx = np.arange(k)
    return np.exp2(a[idx // 512, idx % 128 // 32])


BF16 = ml_dtypes.bfloat16


def bf(x):
    return np.asarray(x, np.float32).astype(BF16)


def f64(x):
    return np.asarray(x).astype(np.float64)


E2M1 = np.array([0.0, 0.5, 1.0, 1.5, 2.0, 3.0, 4.0, 6.0, -0.0, -0.5, -1.0, -1.5, -2.0, -3.0, -4.0, -6.0])


def pack_weight(w, fmt):
    k, n = w.shape
    w = f64(bf(w)).reshape(k // 32, 32, n)
    amax = np.abs(w).max(1)
    if fmt == "e4m3":
        byte = np.frexp(amax)[1] - 1 + 127 - 7
    else:
        mant, ex = np.frexp(amax / 6.0)
        byte = np.where(mant > 0.5, ex, ex - 1) + 127
    byte = np.clip(np.where(amax > 0, byte, 1), 1, 254)
    scaled = (w * np.exp2(127.0 - byte)[:, None, :]).reshape(k, n).astype(np.float32)
    by_word = np.ascontiguousarray(scaled.reshape(k // 512, 128, 4, n).transpose(0, 1, 3, 2))
    if fmt == "e4m3":
        words = by_word.astype(ml_dtypes.float8_e4m3fn).view(np.uint8)
    else:
        c = by_word.astype(ml_dtypes.float4_e2m1fn).view(np.uint8) & 0xF
        words = c[..., 0::2] | (c[..., 1::2] << 4)
    return np.ascontiguousarray(words), np.ascontiguousarray(byte.astype(np.uint8).reshape(k // 512, 16, n))


def unpack_weight(words, scales, fmt):
    g, p, n, _ = words.shape
    if fmt == "e4m3":
        vals = np.ascontiguousarray(words).view(ml_dtypes.float8_e4m3fn).astype(np.float64)
    else:
        nib = np.empty((g, p, n, 4), np.uint8)
        nib[..., 0::2] = words & 0xF
        nib[..., 1::2] = words >> 4
        vals = E2M1[nib]
    vals = vals * np.repeat(np.exp2(scales.astype(np.float64) - 127.0), 8, axis=1)[..., None]
    return vals.transpose(0, 1, 3, 2).reshape(g * 512, n)

def pack4(w):
    words, scales = pack_weight(w, "e2m1")
    return words.reshape(words.shape[0], 128, -1), scales


def unpack4(words, scales):
    return unpack_weight(words.reshape(words.shape[0], 128, -1, 2), scales, "e2m1")


B, F, H, C = 1024, 1024, 512, 10
EPS = 4.0 / 30.0
P_KEEP = 0.95


def setup_inputs():
    s = mx_kscale(F)
    ns = EPS / (6.0 * np.sqrt(H))
    x1 = bf(np.random.standard_normal((B, F)) * s)
    x2 = bf(np.random.standard_normal((B, F)) * s)
    W1_words, W1_scales = pack4(np.random.standard_normal((F, H)) / np.sqrt(F) / s[:, None])
    b1 = bf(np.random.standard_normal(H) * 0.3)
    W2_words, W2_scales = pack4(np.random.standard_normal((F, H)) / np.sqrt(F) / s[:, None])
    b2 = bf(np.random.standard_normal(H) * 0.3)
    noise_std = bf(np.random.laplace(size=(B, H)) * ns)
    rr_uniform = bf(np.random.uniform(size=H))
    return {"x1": x1,
            "x2": x2,
            "W1_words": W1_words,
            "W1_scales": W1_scales,
            "b1": b1,
            "W2_words": W2_words,
            "W2_scales": W2_scales,
            "b2": b2,
            "noise_std": noise_std,
            "rr_uniform": rr_uniform}


def reference(x1, x2, W1_words, W1_scales, b1, W2_words, W2_scales, b2, noise_std, rr_uniform):
    out1 = (mxq(f64(x1), 1, "e4m3") @ unpack4(W1_words, W1_scales)) + f64(b1)
    one_norm = np.sum(np.abs(out1), axis=1)
    sensitivity = np.max(one_norm) - np.min(one_norm)
    noise_mul = sensitivity / EPS
    out1 = out1 + f64(noise_std) * noise_mul
    rr_mask = np.where(f64(rr_uniform) < P_KEEP, 1.0, 0.0)
    out1 = out1 * rr_mask
    out2 = (mxq(f64(x2), 1, "e4m3") @ unpack4(W2_words, W2_scales)) + f64(b2)
    return np.minimum(out1, out2)

@@ -1,0 +1,224 @@
+from contextlib import ExitStack
+
+import concourse.mybir as mybir
+from concourse.masks import make_identity
+
+F32 = mybir.dt.float32
+BF16 = mybir.dt.bfloat16
+I32 = mybir.dt.int32
+U32 = mybir.dt.uint32
+U8 = mybir.dt.uint8
+FP8X4 = mybir.dt.float8_e4m3fn_x4
+FP4X4 = mybir.dt.float4_e2m1fn_x4
+ALU = mybir.AluOpType
+ACT = mybir.ActivationFunctionType
+AX = mybir.AxisListType
+
+P = 128
+B, F, H = 1024, 1024, 512
+PACK = 4
+K_PASS = P * PACK
+PASSES = F // K_PASS
+ROW_TILES = B // P
+UNIT_TILES = 2
+UNITS = ROW_TILES // UNIT_TILES
+LAG = 2
+WORD_HALVES = 2
+INV_EPS = 30.0 / 4.0
+P_KEEP = 0.95
+
+FLOPS = 2 * 2 * B * F * H
+
+
+def tile_splitnn_pa_kernel(
+    tc, x1, x2, W1_words, W1_scales, b1, W2_words, W2_scales, b2, noise_std, rr_uniform, out
+):
+    nc = tc.nc
+    x_rows = [x.rearrange("(p t) k -> p t k", t=ROW_TILES) for x in (x1, x2)]
+    noise_rows = noise_std.rearrange("(p t) h -> p t h", t=ROW_TILES)
+    out_rows = out.rearrange("(p t) h -> p t h", t=ROW_TILES)
+
+    with ExitStack() as ctx:
+        const = ctx.enter_context(tc.tile_pool(name="const", bufs=1))
+        data = ctx.enter_context(tc.tile_pool(name="data", bufs=1))
+        stage = ctx.enter_context(tc.tile_pool(name="stage", bufs=3))
+        psum_t = ctx.enter_context(tc.psum_pool(name="psum_t", bufs=4))
+        psum_acc = ctx.enter_context(tc.psum_pool(name="psum_acc", bufs=4))
+        ctx.enter_context(tc.manual_schedule())
+
+        w_words = [const.tile([P, PASSES, 2 * H], U8, name="w_words%d" % c, align_bytes=64) for c in range(2)]
+        w_planes = [const.tile([P, PASSES, H], U8, name="w_planes%d" % c, align_bytes=64) for c in range(2)]
+        x_sb = [
+            [data.tile([P, UNIT_TILES, F], BF16, name="x%d_%d" % (c, j)) for j in range(UNITS)]
+            for c in range(2)
+        ]
+        noise_sb = data.tile([P, ROW_TILES, H], BF16)
+        rows_sb = [data.tile([P, UNIT_TILES, H], F32, name="rows%d" % j) for j in range(UNITS)]
+        norms = const.tile([P, ROW_TILES], F32)
+
+        for c in range(2):
+            nc.vector.memset(w_planes[c][:].bitcast(I32), 0)
+        vec_rows = const.tile([P, 3, H], BF16)
+        nc.vector.memset(vec_rows[:], 0.0)
+        ones = const.tile([P, P], BF16)
+        nc.vector.memset(ones[:], 1.0)
+        table_warmer = const.tile([P, 1], F32)
+        nc.vector.memset(table_warmer[:], 0.0)
+        ident = const.tile([P, P], F32)
+        make_identity(nc, ident[:])
+
+        def load_x(c, j):
+            tiles = slice(j * UNIT_TILES, (j + 1) * UNIT_TILES)
+            nc.sync.dma_start(out=x_sb[c][j][:], in_=x_rows[c][:, tiles, :])
+
+        def load_weight(c, words, scales):
+            plane_words = w_planes[c][:].bitcast(I32)
+            scale_rows = scales.bitcast(I32).rearrange("g (q l) n -> l q g n", l=4)
+            for l in range(4):
+                nc.sync.dma_start(out=plane_words[l:P:32, :, :], in_=scale_rows[l])
+            nc.sync.dma_start(
+                out=w_words[c][:].bitcast(I32), in_=words.bitcast(I32).rearrange("g p b -> p g b")
+            )
+
+        load_x(0, 0)
+        load_weight(0, W1_words, W1_scales)
+        for j in range(1, UNITS):
+            load_x(0, j)
+        load_weight(1, W2_words, W2_scales)
+        load_x(1, 0)
+        load_x(1, 1)
+        nc.sync.dma_start(out=noise_sb[:], in_=noise_rows)
+        load_x(1, 2)
+        load_x(1, 3)
+        for v, vec in enumerate((b1, b2, rr_uniform)):
+            nc.scalar.dma_start(out=vec_rows[0:1, v, :], in_=vec.unsqueeze(0))
+
+        nc.scalar.activation(out=table_warmer[:], in_=table_warmer[:], func=ACT.Abs)
+
+        spread = []
+        for v in range(3):
+            spread_ps = psum_acc.tile([P, H], F32, tag="acc")
+            nc.tensor.matmul(out=spread_ps[:], lhsT=ones[:], rhs=vec_rows[:, v, :], start=True, stop=True)
+            spread.append(spread_ps)
+        b1_all = const.tile([P, H], F32)
+        nc.scalar.copy(out=b1_all[:], in_=spread[0][:])
+        b2_all = const.tile([P, H], F32)
+        nc.scalar.copy(out=b2_all[:], in_=spread[1][:])
+        keep_all = const.tile([P, H], F32)
+        nc.vector.tensor_single_scalar(out=keep_all[:], in_=spread[2][:], scalar=P_KEEP, op=ALU.is_lt)
+
+        def transpose_unit(c, j):
+            grouped = stage.tile([P, UNIT_TILES, PASSES, P, PACK], BF16, align_bytes=64, tag="grouped")
+            for i in range(UNIT_TILES):
+                x_words = x_sb[c][j][:, i, :].bitcast(F32)
+                xt = psum_t.tile([P, PASSES * WORD_HALVES, P], F32, tag="xt")
+                for g in range(PASSES):
+                    first = g * K_PASS // 2
+                    for u in range(WORD_HALVES):
+                        nc.tensor.transpose(
+                            xt[:, g * WORD_HALVES + u, :],
+                            x_words[:, first + u : first + K_PASS // 2 : WORD_HALVES],
+                            ident[:],
+                        )
+                nc.scalar.copy(
+                    out=grouped[:, i, :, :, :].bitcast(F32),
+                    in_=xt[:].rearrange("p (g u) r -> p g r u", u=WORD_HALVES),
+                )
+            return grouped
+
+        def quantise_unit(grouped):
+            codes = stage.tile([P, UNIT_TILES * PASSES * P], U32, align_bytes=64, tag="codes")
+            x_plane = stage.tile([P, UNIT_TILES * PASSES * P], U8, align_bytes=64, tag="x_plane")
+            nc.vector.quantize_mx(
+                out=codes[:].bitcast(FP8X4),
+                scales=x_plane[:],
+                in_=grouped[:].rearrange("p i g r s -> p (i g r s)"),
+            )
+            return codes, x_plane
+
+        def multiply_unit(c, codes, x_plane):
+            products = []
+            for i in range(UNIT_TILES):
+                acc = psum_acc.tile([P, H], F32, tag="acc")
+                for g in range(PASSES):
+                    rows = slice((i * PASSES + g) * P, (i * PASSES + g + 1) * P)
+                    nc.tensor.matmul_mx(
+                        out=acc[:],
+                        lhsT=codes[:, rows].bitcast(FP8X4),
+                        lhsT_scale=x_plane[:, rows],
+                        rhs=w_words[c][:, g, :].bitcast(FP4X4),
+                        rhs_scale=w_planes[c][:, g, :],
+                        start=(g == 0),
+                        stop=(g == PASSES - 1),
+                    )
+                products.append(acc)
+            return products
+
+        def client1_rows(j, products):
+            for i in range(UNIT_TILES):
+                nc.vector.tensor_tensor(out=rows_sb[j][:, i, :], in0=products[i][:], in1=b1_all[:], op=ALU.add)
+                absolute = stage.tile([P, H], BF16, tag="absolute")
+                t = j * UNIT_TILES + i
+                nc.scalar.activation(
+                    out=absolute[:], in_=rows_sb[j][:, i, :], func=ACT.Abs, accum_out=norms[:, t : t + 1]
+                )
+
+        def noise_multiplier():
+            part_max = const.tile([P, 1], F32)
+            nc.vector.tensor_reduce(out=part_max[:], in_=norms[:], axis=AX.X, op=ALU.max)
+            part_min = const.tile([P, 1], F32)
+            nc.vector.tensor_reduce(out=part_min[:], in_=norms[:], axis=AX.X, op=ALU.min)
+            repeated = const.tile([P, 2, P], F32)
+            nc.vector.tensor_copy(out=repeated[:, 0, :], in_=part_max[:, 0:1].to_broadcast([P, P]))
+            nc.vector.tensor_copy(out=repeated[:, 1, :], in_=part_min[:, 0:1].to_broadcast([P, P]))
+            across = psum_t.tile([P, 2, P], F32, tag="xt")
+            nc.tensor.transpose(across[:, 0, :], repeated[:, 0, :], ident[:])
+            nc.tensor.transpose(across[:, 1, :], repeated[:, 1, :], ident[:])
+            all_max = const.tile([P, 1], F32)
+            nc.vector.tensor_reduce(out=all_max[:], in_=across[:, 0, :], axis=AX.X, op=ALU.max)
+            all_min = const.tile([P, 1], F32)
+            nc.vector.tensor_reduce(out=all_min[:], in_=across[:, 1, :], axis=AX.X, op=ALU.min)
+            multiplier = const.tile([P, 1], F32)
+            nc.vector.tensor_scalar(
+                out=multiplier[:], in0=all_max[:], scalar1=all_min[:, 0:1], scalar2=INV_EPS,
+                op0=ALU.subtract, op1=ALU.mult,
+            )
+            return multiplier
+
+        def finish_rows(j, products, multiplier):
+            tiles = slice(j * UNIT_TILES, (j + 1) * UNIT_TILES)
+            c_rows = rows_sb[j]
+            d_rows = [stage.tile([P, H], F32, name="d_rows%d" % i) for i in range(UNIT_TILES)]
+            nc.vector.scalar_tensor_tensor(
+                out=c_rows[:], in0=noise_sb[:, tiles, :], scalar=multiplier[:, 0:1], in1=c_rows[:],
+                op0=ALU.mult, op1=ALU.add,
+            )
+            nc.vector.tensor_tensor(out=d_rows[0][:], in0=products[0][:], in1=b2_all[:], op=ALU.add)
+            nc.vector.tensor_tensor(
+                out=c_rows[:], in0=c_rows[:], in1=keep_all[:].unsqueeze(1).to_broadcast([P, UNIT_TILES, H]),
+                op=ALU.mult,
+            )
+            for i in range(1, UNIT_TILES):
+                nc.vector.tensor_tensor(out=d_rows[i][:], in0=products[i][:], in1=b2_all[:], op=ALU.add)
+            for i in range(UNIT_TILES):
+                nc.vector.tensor_tensor(out=c_rows[:, i, :], in0=c_rows[:, i, :], in1=d_rows[i][:], op=ALU.min)
+            nc.sync.dma_start(out=out_rows[:, tiles, :], in_=c_rows[:])
+
+        units = [(c, j) for c in range(2) for j in range(UNITS)]
+        grouped_of = {}
+        quantised_of = {}
+        multiplier = None
+        for step in range(len(units) + LAG):
+            if step < len(units):
+                grouped_of[step] = transpose_unit(*units[step])
+            if step >= LAG:
+                c, j = units[step - LAG]
+                products = multiply_unit(c, *quantised_of[step - LAG])
+                if c == 0:
+                    client1_rows(j, products)
+                    if j == UNITS - 1:
+                        multiplier = noise_multiplier()
+                else:
+                    finish_rows(j, products, multiplier)
+            if step < len(units):
+                quantised_of[step] = quantise_unit(grouped_of[step])

@@ -22,7 +22,12 @@ PASSES = F // K_PASS
 ROW_TILES = B // P
 UNIT_TILES = 2
 UNITS = ROW_TILES // UNIT_TILES
-LAG = 2
+MOVING = 512
+HALF_TILES = MOVING // P
+HALF_UNITS = HALF_TILES // UNIT_TILES
+HALVES = ROW_TILES // HALF_TILES
+LAG = HALF_UNITS
+H_SLICES = H // P
 WORD_HALVES = 2
 INV_EPS = 30.0 / 4.0
 P_KEEP = 0.95
@@ -55,6 +60,14 @@ def tile_splitnn_pa_kernel(
         noise_sb = data.tile([P, ROW_TILES, H], BF16)
         rows_sb = [data.tile([P, UNIT_TILES, H], F32, name="rows%d" % j) for j in range(UNITS)]
         norms = const.tile([P, ROW_TILES], F32)
+        x_codes = [
+            [data.tile([P, PASSES, MOVING], U32, name="x_codes%d_%d" % (c, n), align_bytes=64) for n in range(HALVES)]
+            for c in range(2)
+        ]
+        x_planes = [
+            [data.tile([P, PASSES, MOVING], U8, name="x_planes%d_%d" % (c, n), align_bytes=64) for n in range(HALVES)]
+            for c in range(2)
+        ]
 
         for c in range(2):
             nc.vector.memset(w_planes[c][:].bitcast(I32), 0)
@@ -102,13 +115,20 @@ def tile_splitnn_pa_kernel(
             spread.append(spread_ps)
         b1_all = const.tile([P, H], F32)
         nc.scalar.copy(out=b1_all[:], in_=spread[0][:])
-        b2_all = const.tile([P, H], F32)
-        nc.scalar.copy(out=b2_all[:], in_=spread[1][:])
         keep_all = const.tile([P, H], F32)
         nc.vector.tensor_single_scalar(out=keep_all[:], in_=spread[2][:], scalar=P_KEEP, op=ALU.is_lt)
+        b2_diagonal = const.tile([P, H_SLICES, P], F32)
+        nc.vector.tensor_tensor(
+            out=b2_diagonal[:],
+            in0=spread[1][:].rearrange("p (a m) -> p a m", m=P),
+            in1=ident[:].unsqueeze(1).to_broadcast([P, H_SLICES, P]),
+            op=ALU.mult,
+        )
+        b2_cols = const.tile([P, H_SLICES], F32)
+        nc.vector.tensor_reduce(out=b2_cols[:], in_=b2_diagonal[:], axis=AX.X, op=ALU.add)
 
         def transpose_unit(c, j):
-            grouped = stage.tile([P, UNIT_TILES, PASSES, P, PACK], BF16, align_bytes=64, tag="grouped")
+            grouped = stage.tile([P, PASSES, UNIT_TILES, P, PACK], BF16, align_bytes=64, tag="grouped")
             for i in range(UNIT_TILES):
                 x_words = x_sb[c][j][:, i, :].bitcast(F32)
                 xt = psum_t.tile([P, PASSES * WORD_HALVES, P], F32, tag="xt")
@@ -121,44 +141,39 @@ def tile_splitnn_pa_kernel(
                             ident[:],
                         )
                 nc.scalar.copy(
-                    out=grouped[:, i, :, :, :].bitcast(F32),
+                    out=grouped[:, :, i, :, :].bitcast(F32),
                     in_=xt[:].rearrange("p (g u) r -> p g r u", u=WORD_HALVES),
                 )
             return grouped
 
-        def quantise_unit(grouped):
-            codes = stage.tile([P, UNIT_TILES * PASSES * P], U32, align_bytes=64, tag="codes")
-            x_plane = stage.tile([P, UNIT_TILES * PASSES * P], U8, align_bytes=64, tag="x_plane")
-            nc.vector.quantize_mx(
-                out=codes[:].bitcast(FP8X4),
-                scales=x_plane[:],
-                in_=grouped[:].rearrange("p i g r s -> p (i g r s)"),
-            )
-            return codes, x_plane
+        def quantise_unit(c, j, grouped):
+            half = j // HALF_UNITS
+            rows = slice((j % HALF_UNITS) * UNIT_TILES * P, (j % HALF_UNITS + 1) * UNIT_TILES * P)
+            for g in range(PASSES):
+                nc.vector.quantize_mx(
+                    out=x_codes[c][half][:, g, rows].bitcast(FP8X4),
+                    scales=x_planes[c][half][:, g, rows],
+                    in_=grouped[:, g, :, :, :].rearrange("p i r s -> p (i r s)"),
+                )
 
-        def multiply_unit(c, codes, x_plane):
-            products = []
+        def client1_rows(j):
+            half = j // HALF_UNITS
             for i in range(UNIT_TILES):
+                t = j * UNIT_TILES + i
+                rows = slice((t % HALF_TILES) * P, (t % HALF_TILES + 1) * P)
                 acc = psum_acc.tile([P, H], F32, tag="acc")
                 for g in range(PASSES):
-                    rows = slice((i * PASSES + g) * P, (i * PASSES + g + 1) * P)
                     nc.tensor.matmul_mx(
                         out=acc[:],
-                        lhsT=codes[:, rows].bitcast(FP8X4),
-                        lhsT_scale=x_plane[:, rows],
-                        rhs=w_words[c][:, g, :].bitcast(FP4X4),
-                        rhs_scale=w_planes[c][:, g, :],
+                        lhsT=x_codes[0][half][:, g, rows].bitcast(FP8X4),
+                        lhsT_scale=x_planes[0][half][:, g, rows],
+                        rhs=w_words[0][:, g, :].bitcast(FP4X4),
+                        rhs_scale=w_planes[0][:, g, :],
                         start=(g == 0),
                         stop=(g == PASSES - 1),
                     )
-                products.append(acc)
-            return products
-
-        def client1_rows(j, products):
-            for i in range(UNIT_TILES):
-                nc.vector.tensor_tensor(out=rows_sb[j][:, i, :], in0=products[i][:], in1=b1_all[:], op=ALU.add)
+                nc.vector.tensor_tensor(out=rows_sb[j][:, i, :], in0=acc[:], in1=b1_all[:], op=ALU.add)
                 absolute = stage.tile([P, H], BF16, tag="absolute")
-                t = j * UNIT_TILES + i
                 nc.scalar.activation(
                     out=absolute[:], in_=rows_sb[j][:, i, :], func=ACT.Abs, accum_out=norms[:, t : t + 1]
                 )
@@ -185,40 +200,68 @@ def tile_splitnn_pa_kernel(
             )
             return multiplier
 
-        def finish_rows(j, products, multiplier):
+        def client2_columns(half):
+            d_cols = stage.tile([P, H_SLICES, MOVING], F32, tag="d_cols", bufs=2)
+            for a in range(H_SLICES):
+                acc = psum_acc.tile([P, MOVING], F32, tag="acc")
+                for g in range(PASSES):
+                    nc.tensor.matmul_mx(
+                        out=acc[:],
+                        lhsT=w_words[1][:, g, 2 * P * a : 2 * P * (a + 1)].bitcast(FP4X4),
+                        lhsT_scale=w_planes[1][:, g, P * a : P * (a + 1)],
+                        rhs=x_codes[1][half][:, g, :].bitcast(FP8X4),
+                        rhs_scale=x_planes[1][half][:, g, :],
+                        start=(g == 0),
+                        stop=(g == PASSES - 1),
+                    )
+                nc.scalar.activation(
+                    out=d_cols[:, a, :], in_=acc[:], func=ACT.Identity, bias=b2_cols[:, a : a + 1]
+                )
+            return d_cols
+
+        def noisy_rows(j, multiplier):
             tiles = slice(j * UNIT_TILES, (j + 1) * UNIT_TILES)
-            c_rows = rows_sb[j]
-            d_rows = [stage.tile([P, H], F32, name="d_rows%d" % i) for i in range(UNIT_TILES)]
             nc.vector.scalar_tensor_tensor(
-                out=c_rows[:], in0=noise_sb[:, tiles, :], scalar=multiplier[:, 0:1], in1=c_rows[:],
+                out=rows_sb[j][:], in0=noise_sb[:, tiles, :], scalar=multiplier[:, 0:1], in1=rows_sb[j][:],
                 op0=ALU.mult, op1=ALU.add,
             )
-            nc.vector.tensor_tensor(out=d_rows[0][:], in0=products[0][:], in1=b2_all[:], op=ALU.add)
             nc.vector.tensor_tensor(
-                out=c_rows[:], in0=c_rows[:], in1=keep_all[:].unsqueeze(1).to_broadcast([P, UNIT_TILES, H]),
-                op=ALU.mult,
+                out=rows_sb[j][:], in0=rows_sb[j][:],
+                in1=keep_all[:].unsqueeze(1).to_broadcast([P, UNIT_TILES, H]), op=ALU.mult,
             )
-            for i in range(1, UNIT_TILES):
-                nc.vector.tensor_tensor(out=d_rows[i][:], in0=products[i][:], in1=b2_all[:], op=ALU.add)
-            for i in range(UNIT_TILES):
-                nc.vector.tensor_tensor(out=c_rows[:, i, :], in0=c_rows[:, i, :], in1=d_rows[i][:], op=ALU.min)
-            nc.sync.dma_start(out=out_rows[:, tiles, :], in_=c_rows[:])
 
-        units = [(c, j) for c in range(2) for j in range(UNITS)]
-        grouped_of = {}
-        quantised_of = {}
-        multiplier = None
-        for step in range(len(units) + LAG):
-            if step < len(units):
-                grouped_of[step] = transpose_unit(*units[step])
+        def finish_rows(j, d_cols):
+            for i in range(UNIT_TILES):
+                t = j * UNIT_TILES + i
+                rows = slice((t % HALF_TILES) * P, (t % HALF_TILES + 1) * P)
+                d_rows = psum_t.tile([P, H_SLICES, P], F32, tag="xt")
+                for a in range(H_SLICES):
+                    nc.tensor.transpose(d_rows[:, a, :], d_cols[:, a, rows], ident[:])
+                nc.vector.tensor_tensor(
+                    out=rows_sb[j][:, i, :], in0=rows_sb[j][:, i, :],
+                    in1=d_rows[:].rearrange("p a m -> p (a m)"), op=ALU.min,
+                )
+            tiles = slice(j * UNIT_TILES, (j + 1) * UNIT_TILES)
+            nc.sync.dma_start(out=out_rows[:, tiles, :], in_=rows_sb[j][:])
+
+        ahead = [(0, j) for j in range(UNITS)] + [(1, j) for j in range(HALF_UNITS)]
+        for step, (c, j) in enumerate(ahead):
+            grouped = transpose_unit(c, j)
             if step >= LAG:
-                c, j = units[step - LAG]
-                products = multiply_unit(c, *quantised_of[step - LAG])
-                if c == 0:
-                    client1_rows(j, products)
-                    if j == UNITS - 1:
-                        multiplier = noise_multiplier()
-                else:
-                    finish_rows(j, products, multiplier)
-            if step < len(units):
-                quantised_of[step] = quantise_unit(grouped_of[step])
+                client1_rows(step - LAG)
+            quantise_unit(c, j, grouped)
+        multiplier = noise_multiplier()
+
+        for half in range(HALVES):
+            mine = range(half * HALF_UNITS, (half + 1) * HALF_UNITS)
+            d_cols = client2_columns(half)
+            if half + 1 < HALVES:
+                following = range((half + 1) * HALF_UNITS, (half + 2) * HALF_UNITS)
+                grouped_of = [transpose_unit(1, j) for j in following]
+            for j in mine:
+                noisy_rows(j, multiplier)
+            if half + 1 < HALVES:
+                for j, grouped in zip(following, grouped_of):
+                    quantise_unit(1, j, grouped)
+            for j in mine:
+                finish_rows(j, d_cols)

@@ -46,17 +46,14 @@ def tile_splitnn_pa_kernel(
     with ExitStack() as ctx:
         const = ctx.enter_context(tc.tile_pool(name="const", bufs=1))
         data = ctx.enter_context(tc.tile_pool(name="data", bufs=1))
-        stage = ctx.enter_context(tc.tile_pool(name="stage", bufs=3))
+        stage = ctx.enter_context(tc.tile_pool(name="stage", bufs=UNITS))
         psum_t = ctx.enter_context(tc.psum_pool(name="psum_t", bufs=4))
         psum_acc = ctx.enter_context(tc.psum_pool(name="psum_acc", bufs=4))
         ctx.enter_context(tc.manual_schedule())
 
         w_words = [const.tile([P, PASSES, 2 * H], U8, name="w_words%d" % c, align_bytes=64) for c in range(2)]
         w_planes = [const.tile([P, PASSES, H], U8, name="w_planes%d" % c, align_bytes=64) for c in range(2)]
-        x_sb = [
-            [data.tile([P, UNIT_TILES, F], BF16, name="x%d_%d" % (c, j)) for j in range(UNITS)]
-            for c in range(2)
-        ]
+        x_sb = [[data.tile([P, F], BF16, name="x%d_%d" % (c, t)) for t in range(ROW_TILES)] for c in range(2)]
         noise_sb = data.tile([P, ROW_TILES, H], BF16)
         rows_sb = [data.tile([P, UNIT_TILES, H], F32, name="rows%d" % j) for j in range(UNITS)]
         norms = const.tile([P, ROW_TILES], F32)
@@ -80,9 +77,9 @@ def tile_splitnn_pa_kernel(
         ident = const.tile([P, P], F32)
         make_identity(nc, ident[:])
 
-        def load_x(c, j):
-            tiles = slice(j * UNIT_TILES, (j + 1) * UNIT_TILES)
-            nc.sync.dma_start(out=x_sb[c][j][:], in_=x_rows[c][:, tiles, :])
+        def load_x(c, tiles):
+            for t in tiles:
+                nc.sync.dma_start(out=x_sb[c][t][:], in_=x_rows[c][:, t, :])
 
         def load_weight(c, words, scales):
             plane_words = w_planes[c][:].bitcast(I32)
@@ -93,44 +90,43 @@ def tile_splitnn_pa_kernel(
                 out=w_words[c][:].bitcast(I32), in_=words.bitcast(I32).rearrange("g p b -> p g b")
             )
 
-        load_x(0, 0)
+        load_x(0, range(UNIT_TILES))
         load_weight(0, W1_words, W1_scales)
-        for j in range(1, UNITS):
-            load_x(0, j)
+        load_x(0, range(UNIT_TILES, ROW_TILES))
         load_weight(1, W2_words, W2_scales)
-        load_x(1, 0)
-        load_x(1, 1)
+        load_x(1, range(HALF_TILES))
         nc.sync.dma_start(out=noise_sb[:], in_=noise_rows)
-        load_x(1, 2)
-        load_x(1, 3)
+        load_x(1, range(HALF_TILES, ROW_TILES))
         for v, vec in enumerate((b1, b2, rr_uniform)):
             nc.scalar.dma_start(out=vec_rows[0:1, v, :], in_=vec.unsqueeze(0))
 
         nc.scalar.activation(out=table_warmer[:], in_=table_warmer[:], func=ACT.Abs)
 
-        spread = []
-        for v in range(3):
-            spread_ps = psum_acc.tile([P, H], F32, tag="acc")
-            nc.tensor.matmul(out=spread_ps[:], lhsT=ones[:], rhs=vec_rows[:, v, :], start=True, stop=True)
-            spread.append(spread_ps)
         b1_all = const.tile([P, H], F32)
-        nc.scalar.copy(out=b1_all[:], in_=spread[0][:])
         keep_all = const.tile([P, H], F32)
-        nc.vector.tensor_single_scalar(out=keep_all[:], in_=spread[2][:], scalar=P_KEEP, op=ALU.is_lt)
-        b2_diagonal = const.tile([P, H_SLICES, P], F32)
-        nc.vector.tensor_tensor(
-            out=b2_diagonal[:],
-            in0=spread[1][:].rearrange("p (a m) -> p a m", m=P),
-            in1=ident[:].unsqueeze(1).to_broadcast([P, H_SLICES, P]),
-            op=ALU.mult,
-        )
         b2_cols = const.tile([P, H_SLICES], F32)
-        nc.vector.tensor_reduce(out=b2_cols[:], in_=b2_diagonal[:], axis=AX.X, op=ALU.add)
+
+        def spread_vectors():
+            spread = []
+            for v in range(3):
+                spread_ps = psum_acc.tile([P, H], F32, tag="acc")
+                nc.tensor.matmul(out=spread_ps[:], lhsT=ones[:], rhs=vec_rows[:, v, :], start=True, stop=True)
+                spread.append(spread_ps)
+            nc.scalar.copy(out=b1_all[:], in_=spread[0][:])
+            nc.vector.tensor_single_scalar(out=keep_all[:], in_=spread[2][:], scalar=P_KEEP, op=ALU.is_lt)
+            b2_diagonal = const.tile([P, H_SLICES, P], F32)
+            nc.vector.tensor_tensor(
+                out=b2_diagonal[:],
+                in0=spread[1][:].rearrange("p (a m) -> p a m", m=P),
+                in1=ident[:].unsqueeze(1).to_broadcast([P, H_SLICES, P]),
+                op=ALU.mult,
+            )
+            nc.vector.tensor_reduce(out=b2_cols[:], in_=b2_diagonal[:], axis=AX.X, op=ALU.add)
 
         def transpose_unit(c, j):
             grouped = stage.tile([P, PASSES, UNIT_TILES, P, PACK], BF16, align_bytes=64, tag="grouped")
             for i in range(UNIT_TILES):
-                x_words = x_sb[c][j][:, i, :].bitcast(F32)
+                x_words = x_sb[c][j * UNIT_TILES + i][:].bitcast(F32)
                 xt = psum_t.tile([P, PASSES * WORD_HALVES, P], F32, tag="xt")
                 for g in range(PASSES):
                     first = g * K_PASS // 2
@@ -186,7 +182,7 @@ def tile_splitnn_pa_kernel(
             repeated = const.tile([P, 2, P], F32)
             nc.vector.tensor_copy(out=repeated[:, 0, :], in_=part_max[:, 0:1].to_broadcast([P, P]))
             nc.vector.tensor_copy(out=repeated[:, 1, :], in_=part_min[:, 0:1].to_broadcast([P, P]))
-            across = psum_t.tile([P, 2, P], F32, tag="xt")
+            across = psum_acc.tile([P, 2, P], F32, tag="acc")
             nc.tensor.transpose(across[:, 0, :], repeated[:, 0, :], ident[:])
             nc.tensor.transpose(across[:, 1, :], repeated[:, 1, :], ident[:])
             all_max = const.tile([P, 1], F32)
@@ -241,27 +237,31 @@ def tile_splitnn_pa_kernel(
                     out=rows_sb[j][:, i, :], in0=rows_sb[j][:, i, :],
                     in1=d_rows[:].rearrange("p a m -> p (a m)"), op=ALU.min,
                 )
-            tiles = slice(j * UNIT_TILES, (j + 1) * UNIT_TILES)
-            nc.sync.dma_start(out=out_rows[:, tiles, :], in_=rows_sb[j][:])
+                nc.sync.dma_start(out=out_rows[:, t, :], in_=rows_sb[j][:, i, :])
 
-        ahead = [(0, j) for j in range(UNITS)] + [(1, j) for j in range(HALF_UNITS)]
-        for step, (c, j) in enumerate(ahead):
-            grouped = transpose_unit(c, j)
-            if step >= LAG:
-                client1_rows(step - LAG)
-            quantise_unit(c, j, grouped)
+        for j in range(LAG):
+            quantise_unit(0, j, transpose_unit(0, j))
+            if j == 0:
+                spread_vectors()
+        for j in range(UNITS):
+            if j + LAG < UNITS:
+                grouped = transpose_unit(0, j + LAG)
+            client1_rows(j)
+            if j + LAG < UNITS:
+                quantise_unit(0, j + LAG, grouped)
+
+        grouped_of = [transpose_unit(1, j) for j in range(HALF_UNITS)]
         multiplier = noise_multiplier()
-
+        grouped_of.extend([transpose_unit(1, j) for j in range(HALF_UNITS, UNITS)])
+        for j in range(HALF_UNITS):
+            quantise_unit(1, j, grouped_of[j])
         for half in range(HALVES):
             mine = range(half * HALF_UNITS, (half + 1) * HALF_UNITS)
             d_cols = client2_columns(half)
-            if half + 1 < HALVES:
-                following = range((half + 1) * HALF_UNITS, (half + 2) * HALF_UNITS)
-                grouped_of = [transpose_unit(1, j) for j in following]
             for j in mine:
                 noisy_rows(j, multiplier)
             if half + 1 < HALVES:
-                for j, grouped in zip(following, grouped_of):
-                    quantise_unit(1, j, grouped)
+                for j in range((half + 1) * HALF_UNITS, (half + 2) * HALF_UNITS):
+                    quantise_unit(1, j, grouped_of[j])
             for j in mine:
                 finish_rows(j, d_cols)

@@ -136,7 +136,8 @@ def tile_splitnn_pa_kernel(
                             x_words[:, first + u : first + K_PASS // 2 : WORD_HALVES],
                             ident[:],
                         )
-                nc.scalar.copy(
+                copy_out = nc.vector.tensor_copy if (c == 0 and i % 2 == 1) else nc.scalar.copy
+                copy_out(
                     out=grouped[:, :, i, :, :].bitcast(F32),
                     in_=xt[:].rearrange("p (g u) r -> p g r u", u=WORD_HALVES),
                 )
@@ -215,16 +216,18 @@ def tile_splitnn_pa_kernel(
                 )
             return d_cols
 
-        def noisy_rows(j, multiplier):
-            tiles = slice(j * UNIT_TILES, (j + 1) * UNIT_TILES)
-            nc.vector.scalar_tensor_tensor(
-                out=rows_sb[j][:], in0=noise_sb[:, tiles, :], scalar=multiplier[:, 0:1], in1=rows_sb[j][:],
-                op0=ALU.mult, op1=ALU.add,
-            )
-            nc.vector.tensor_tensor(
-                out=rows_sb[j][:], in0=rows_sb[j][:],
-                in1=keep_all[:].unsqueeze(1).to_broadcast([P, UNIT_TILES, H]), op=ALU.mult,
-            )
+        def noisy_rows(units, multiplier):
+            for j in units:
+                tiles = slice(j * UNIT_TILES, (j + 1) * UNIT_TILES)
+                nc.vector.scalar_tensor_tensor(
+                    out=rows_sb[j][:], in0=noise_sb[:, tiles, :], scalar=multiplier[:, 0:1], in1=rows_sb[j][:],
+                    op0=ALU.mult, op1=ALU.add,
+                )
+            for j in units:
+                nc.vector.tensor_tensor(
+                    out=rows_sb[j][:], in0=rows_sb[j][:],
+                    in1=keep_all[:].unsqueeze(1).to_broadcast([P, UNIT_TILES, H]), op=ALU.mult,
+                )
 
         def finish_rows(j, d_cols):
             for i in range(UNIT_TILES):
@@ -258,8 +261,7 @@ def tile_splitnn_pa_kernel(
         for half in range(HALVES):
             mine = range(half * HALF_UNITS, (half + 1) * HALF_UNITS)
             d_cols = client2_columns(half)
-            for j in mine:
-                noisy_rows(j, multiplier)
+            noisy_rows(mine, multiplier)
             if half + 1 < HALVES:
                 for j in range((half + 1) * HALF_UNITS, (half + 2) * HALF_UNITS):
                     quantise_unit(1, j, grouped_of[j])

@@ -47,8 +47,7 @@ def tile_splitnn_pa_kernel(
         const = ctx.enter_context(tc.tile_pool(name="const", bufs=1))
         data = ctx.enter_context(tc.tile_pool(name="data", bufs=1))
         stage = ctx.enter_context(tc.tile_pool(name="stage", bufs=UNITS))
-        psum_t = ctx.enter_context(tc.psum_pool(name="psum_t", bufs=4))
-        psum_acc = ctx.enter_context(tc.psum_pool(name="psum_acc", bufs=4))
+        psum = ctx.enter_context(tc.psum_pool(name="psum", bufs=8))
         ctx.enter_context(tc.manual_schedule())
 
         w_words = [const.tile([P, PASSES, 2 * H], U8, name="w_words%d" % c, align_bytes=64) for c in range(2)]
@@ -90,9 +89,9 @@ def tile_splitnn_pa_kernel(
                 out=w_words[c][:].bitcast(I32), in_=words.bitcast(I32).rearrange("g p b -> p g b")
             )
 
-        load_x(0, range(UNIT_TILES))
+        load_x(0, range(HALF_TILES))
         load_weight(0, W1_words, W1_scales)
-        load_x(0, range(UNIT_TILES, ROW_TILES))
+        load_x(0, range(HALF_TILES, ROW_TILES))
         load_weight(1, W2_words, W2_scales)
         load_x(1, range(HALF_TILES))
         nc.sync.dma_start(out=noise_sb[:], in_=noise_rows)
@@ -103,31 +102,29 @@ def tile_splitnn_pa_kernel(
         nc.scalar.activation(out=table_warmer[:], in_=table_warmer[:], func=ACT.Abs)
 
         b1_all = const.tile([P, H], F32)
-        keep_all = const.tile([P, H], F32)
-        b2_cols = const.tile([P, H_SLICES], F32)
+        cols = const.tile([P, 2, H_SLICES], F32)
+        b2_cols = cols[:, 0, :]
+        keep_cols = const.tile([P, H_SLICES], F32)
 
         def spread_vectors():
-            spread = []
-            for v in range(3):
-                spread_ps = psum_acc.tile([P, H], F32, tag="acc")
-                nc.tensor.matmul(out=spread_ps[:], lhsT=ones[:], rhs=vec_rows[:, v, :], start=True, stop=True)
-                spread.append(spread_ps)
-            nc.scalar.copy(out=b1_all[:], in_=spread[0][:])
-            nc.vector.tensor_single_scalar(out=keep_all[:], in_=spread[2][:], scalar=P_KEEP, op=ALU.is_lt)
-            b2_diagonal = const.tile([P, H_SLICES, P], F32)
-            nc.vector.tensor_tensor(
-                out=b2_diagonal[:],
-                in0=spread[1][:].rearrange("p (a m) -> p a m", m=P),
-                in1=ident[:].unsqueeze(1).to_broadcast([P, H_SLICES, P]),
-                op=ALU.mult,
-            )
-            nc.vector.tensor_reduce(out=b2_cols[:], in_=b2_diagonal[:], axis=AX.X, op=ALU.add)
+            spread_ps = psum.tile([P, H], F32, tag="bank")
+            nc.tensor.matmul(out=spread_ps[:], lhsT=ones[:], rhs=vec_rows[:, 0, :], start=True, stop=True)
+            nc.scalar.copy(out=b1_all[:], in_=spread_ps[:])
+            cols_ps = psum.tile([P, 2, H_SLICES], F32, tag="bank")
+            for v in range(2):
+                for a in range(H_SLICES):
+                    nc.tensor.matmul(
+                        out=cols_ps[:, v, a : a + 1], lhsT=vec_rows[:, v + 1, a * P : (a + 1) * P],
+                        rhs=ones[:, 0:1], start=True, stop=True,
+                    )
+            nc.scalar.copy(out=cols[:], in_=cols_ps[:])
+            nc.vector.tensor_single_scalar(out=keep_cols[:], in_=cols[:, 1, :], scalar=P_KEEP, op=ALU.is_lt)
 
         def transpose_unit(c, j):
             grouped = stage.tile([P, PASSES, UNIT_TILES, P, PACK], BF16, align_bytes=64, tag="grouped")
             for i in range(UNIT_TILES):
                 x_words = x_sb[c][j * UNIT_TILES + i][:].bitcast(F32)
-                xt = psum_t.tile([P, PASSES * WORD_HALVES, P], F32, tag="xt")
+                xt = psum.tile([P, PASSES * WORD_HALVES, P], F32, tag="bank")
                 for g in range(PASSES):
                     first = g * K_PASS // 2
                     for u in range(WORD_HALVES):
@@ -136,7 +133,7 @@ def tile_splitnn_pa_kernel(
                             x_words[:, first + u : first + K_PASS // 2 : WORD_HALVES],
                             ident[:],
                         )
-                copy_out = nc.vector.tensor_copy if (c == 0 and i % 2 == 1) else nc.scalar.copy
+                copy_out = nc.vector.tensor_copy if (c == 0 and i % 2 == 1 and j < HALF_UNITS) else nc.scalar.copy
                 copy_out(
                     out=grouped[:, :, i, :, :].bitcast(F32),
                     in_=xt[:].rearrange("p (g u) r -> p g r u", u=WORD_HALVES),
@@ -158,7 +155,7 @@ def tile_splitnn_pa_kernel(
             for i in range(UNIT_TILES):
                 t = j * UNIT_TILES + i
                 rows = slice((t % HALF_TILES) * P, (t % HALF_TILES + 1) * P)
-                acc = psum_acc.tile([P, H], F32, tag="acc")
+                acc = psum.tile([P, H], F32, tag="bank")
                 for g in range(PASSES):
                     nc.tensor.matmul_mx(
                         out=acc[:],
@@ -183,7 +180,7 @@ def tile_splitnn_pa_kernel(
             repeated = const.tile([P, 2, P], F32)
             nc.vector.tensor_copy(out=repeated[:, 0, :], in_=part_max[:, 0:1].to_broadcast([P, P]))
             nc.vector.tensor_copy(out=repeated[:, 1, :], in_=part_min[:, 0:1].to_broadcast([P, P]))
-            across = psum_acc.tile([P, 2, P], F32, tag="acc")
+            across = psum.tile([P, 2, P], F32, tag="bank")
             nc.tensor.transpose(across[:, 0, :], repeated[:, 0, :], ident[:])
             nc.tensor.transpose(across[:, 1, :], repeated[:, 1, :], ident[:])
             all_max = const.tile([P, 1], F32)
@@ -200,7 +197,7 @@ def tile_splitnn_pa_kernel(
         def client2_columns(half):
             d_cols = stage.tile([P, H_SLICES, MOVING], F32, tag="d_cols", bufs=2)
             for a in range(H_SLICES):
-                acc = psum_acc.tile([P, MOVING], F32, tag="acc")
+                acc = psum.tile([P, MOVING], F32, tag="bank")
                 for g in range(PASSES):
                     nc.tensor.matmul_mx(
                         out=acc[:],
@@ -216,31 +213,34 @@ def tile_splitnn_pa_kernel(
                 )
             return d_cols
 
-        def noisy_rows(units, multiplier):
-            for j in units:
-                tiles = slice(j * UNIT_TILES, (j + 1) * UNIT_TILES)
+        def noisy_rows(j, multiplier):
+            tiles = slice(j * UNIT_TILES, (j + 1) * UNIT_TILES)
+            nc.vector.scalar_tensor_tensor(
+                out=rows_sb[j][:], in0=noise_sb[:, tiles, :], scalar=multiplier[:, 0:1], in1=rows_sb[j][:],
+                op0=ALU.mult, op1=ALU.add,
+            )
+
+        def fuse_columns(half, d_cols):
+            for a in range(H_SLICES):
+                c_cols = psum.tile([P, HALF_TILES, P], F32, tag="bank")
+                for i in range(HALF_TILES):
+                    t = half * HALF_TILES + i
+                    nc.tensor.transpose(
+                        c_cols[:, i, :], rows_sb[t // UNIT_TILES][:, t % UNIT_TILES, a * P : (a + 1) * P], ident[:]
+                    )
                 nc.vector.scalar_tensor_tensor(
-                    out=rows_sb[j][:], in0=noise_sb[:, tiles, :], scalar=multiplier[:, 0:1], in1=rows_sb[j][:],
-                    op0=ALU.mult, op1=ALU.add,
-                )
-            for j in units:
-                nc.vector.tensor_tensor(
-                    out=rows_sb[j][:], in0=rows_sb[j][:],
-                    in1=keep_all[:].unsqueeze(1).to_broadcast([P, UNIT_TILES, H]), op=ALU.mult,
+                    out=d_cols[:, a, :], in0=c_cols[:].rearrange("p i r -> p (i r)"), scalar=keep_cols[:, a : a + 1],
+                    in1=d_cols[:, a, :], op0=ALU.mult, op1=ALU.min,
                 )
 
-        def finish_rows(j, d_cols):
-            for i in range(UNIT_TILES):
-                t = j * UNIT_TILES + i
-                rows = slice((t % HALF_TILES) * P, (t % HALF_TILES + 1) * P)
-                d_rows = psum_t.tile([P, H_SLICES, P], F32, tag="xt")
-                for a in range(H_SLICES):
-                    nc.tensor.transpose(d_rows[:, a, :], d_cols[:, a, rows], ident[:])
-                nc.vector.tensor_tensor(
-                    out=rows_sb[j][:, i, :], in0=rows_sb[j][:, i, :],
-                    in1=d_rows[:].rearrange("p a m -> p (a m)"), op=ALU.min,
-                )
-                nc.sync.dma_start(out=out_rows[:, t, :], in_=rows_sb[j][:, i, :])
+        def store_rows(t, out_cols, copy_out):
+            rows = slice((t % HALF_TILES) * P, (t % HALF_TILES + 1) * P)
+            out_ps = psum.tile([P, H_SLICES, P], F32, tag="bank")
+            for a in range(H_SLICES):
+                nc.tensor.transpose(out_ps[:, a, :], out_cols[:, a, rows], ident[:])
+            out_sb = stage.tile([P, H], F32, tag="out_sb")
+            copy_out(out=out_sb[:], in_=out_ps[:].rearrange("p a m -> p (a m)"))
+            nc.sync.dma_start(out=out_rows[:, t, :], in_=out_sb[:])
 
         for j in range(LAG):
             quantise_unit(0, j, transpose_unit(0, j))
@@ -255,15 +255,20 @@ def tile_splitnn_pa_kernel(
 
         grouped_of = [transpose_unit(1, j) for j in range(HALF_UNITS)]
         multiplier = noise_multiplier()
-        grouped_of.extend([transpose_unit(1, j) for j in range(HALF_UNITS, UNITS)])
+        noisy_rows(0, multiplier)
+        grouped_of.append(transpose_unit(1, 2))
         for j in range(HALF_UNITS):
             quantise_unit(1, j, grouped_of[j])
-        for half in range(HALVES):
-            mine = range(half * HALF_UNITS, (half + 1) * HALF_UNITS)
-            d_cols = client2_columns(half)
-            noisy_rows(mine, multiplier)
-            if half + 1 < HALVES:
-                for j in range((half + 1) * HALF_UNITS, (half + 2) * HALF_UNITS):
-                    quantise_unit(1, j, grouped_of[j])
-            for j in mine:
-                finish_rows(j, d_cols)
+        noisy_rows(1, multiplier)
+        grouped_of.append(transpose_unit(1, 3))
+        d_cols_of = [client2_columns(0)]
+        for j in range(HALF_UNITS, UNITS):
+            quantise_unit(1, j, grouped_of[j])
+        for j in range(HALF_UNITS, UNITS):
+            noisy_rows(j, multiplier)
+        fuse_columns(0, d_cols_of[0])
+        d_cols_of.append(client2_columns(1))
+        fuse_columns(1, d_cols_of[1])
+        for t in range(ROW_TILES):
+            last_half = t >= HALF_TILES
+            store_rows(t, d_cols_of[t // HALF_TILES], nc.vector.tensor_copy if (last_half and t % 2 == 1) else nc.scalar.copy)

@@ -102,6 +102,7 @@ def tile_splitnn_pa_kernel(
         nc.scalar.activation(out=table_warmer[:], in_=table_warmer[:], func=ACT.Abs)
 
         b1_all = const.tile([P, H], F32)
+        keep_all = const.tile([P, H], F32)
         cols = const.tile([P, 2, H_SLICES], F32)
         b2_cols = cols[:, 0, :]
         keep_cols = const.tile([P, H_SLICES], F32)
@@ -110,6 +111,11 @@ def tile_splitnn_pa_kernel(
             spread_ps = psum.tile([P, H], F32, tag="bank")
             nc.tensor.matmul(out=spread_ps[:], lhsT=ones[:], rhs=vec_rows[:, 0, :], start=True, stop=True)
             nc.scalar.copy(out=b1_all[:], in_=spread_ps[:])
+            u_ps = psum.tile([P, H], F32, tag="bank")
+            nc.tensor.matmul(out=u_ps[:], lhsT=ones[:], rhs=vec_rows[:, 2, :], start=True, stop=True)
+            nc.vector.tensor_single_scalar(out=keep_all[:], in_=u_ps[:], scalar=P_KEEP, op=ALU.is_lt)
+
+        def column_vectors():
             cols_ps = psum.tile([P, 2, H_SLICES], F32, tag="bank")
             for v in range(2):
                 for a in range(H_SLICES):
@@ -118,7 +124,6 @@ def tile_splitnn_pa_kernel(
                         rhs=ones[:, 0:1], start=True, stop=True,
                     )
             nc.scalar.copy(out=cols[:], in_=cols_ps[:])
-            nc.vector.tensor_single_scalar(out=keep_cols[:], in_=cols[:, 1, :], scalar=P_KEEP, op=ALU.is_lt)
 
         def transpose_unit(c, j):
             grouped = stage.tile([P, PASSES, UNIT_TILES, P, PACK], BF16, align_bytes=64, tag="grouped")
@@ -233,6 +238,21 @@ def tile_splitnn_pa_kernel(
                     in1=d_cols[:, a, :], op0=ALU.mult, op1=ALU.min,
                 )
 
+        def mask_rows(j):
+            nc.vector.tensor_tensor(
+                out=rows_sb[j][:], in0=rows_sb[j][:],
+                in1=keep_all[:].unsqueeze(1).to_broadcast([P, UNIT_TILES, H]), op=ALU.mult,
+            )
+
+        def finish_rows(t, d_cols):
+            rows = slice((t % HALF_TILES) * P, (t % HALF_TILES + 1) * P)
+            c_rows = rows_sb[t // UNIT_TILES][:, t % UNIT_TILES, :]
+            d_rows = psum.tile([P, H_SLICES, P], F32, tag="bank")
+            for a in range(H_SLICES):
+                nc.tensor.transpose(d_rows[:, a, :], d_cols[:, a, rows], ident[:])
+            nc.vector.tensor_tensor(out=c_rows, in0=c_rows, in1=d_rows[:].rearrange("p a m -> p (a m)"), op=ALU.min)
+            nc.sync.dma_start(out=out_rows[:, t, :], in_=c_rows)
+
         def store_rows(t, out_cols, copy_out):
             rows = slice((t % HALF_TILES) * P, (t % HALF_TILES + 1) * P)
             out_ps = psum.tile([P, H_SLICES, P], F32, tag="bank")
@@ -253,6 +273,7 @@ def tile_splitnn_pa_kernel(
             if j + LAG < UNITS:
                 quantise_unit(0, j + LAG, grouped)
 
+        column_vectors()
         grouped_of = [transpose_unit(1, j) for j in range(HALF_UNITS)]
         multiplier = noise_multiplier()
         noisy_rows(0, multiplier)
@@ -261,6 +282,7 @@ def tile_splitnn_pa_kernel(
             quantise_unit(1, j, grouped_of[j])
         noisy_rows(1, multiplier)
         grouped_of.append(transpose_unit(1, 3))
+        nc.vector.tensor_single_scalar(out=keep_cols[:], in_=cols[:, 1, :], scalar=P_KEEP, op=ALU.is_lt)
         d_cols_of = [client2_columns(0)]
         for j in range(HALF_UNITS, UNITS):
             quantise_unit(1, j, grouped_of[j])
@@ -268,7 +290,9 @@ def tile_splitnn_pa_kernel(
             noisy_rows(j, multiplier)
         fuse_columns(0, d_cols_of[0])
         d_cols_of.append(client2_columns(1))
-        fuse_columns(1, d_cols_of[1])
-        for t in range(ROW_TILES):
-            last_half = t >= HALF_TILES
-            store_rows(t, d_cols_of[t // HALF_TILES], nc.vector.tensor_copy if (last_half and t % 2 == 1) else nc.scalar.copy)
+        for t in range(HALF_TILES):
+            store_rows(t, d_cols_of[0], nc.scalar.copy)
+        for j in range(HALF_UNITS, UNITS):
+            mask_rows(j)
+        for t in range(HALF_TILES, ROW_TILES):
+            finish_rows(t, d_cols_of[1])

@@ -276,22 +276,22 @@ def tile_splitnn_pa_kernel(
         column_vectors()
         grouped_of = [transpose_unit(1, j) for j in range(HALF_UNITS)]
         multiplier = noise_multiplier()
-        noisy_rows(0, multiplier)
-        grouped_of.append(transpose_unit(1, 2))
         for j in range(HALF_UNITS):
             quantise_unit(1, j, grouped_of[j])
+        noisy_rows(0, multiplier)
+        grouped_of.append(transpose_unit(1, 2))
         noisy_rows(1, multiplier)
         grouped_of.append(transpose_unit(1, 3))
         nc.vector.tensor_single_scalar(out=keep_cols[:], in_=cols[:, 1, :], scalar=P_KEEP, op=ALU.is_lt)
         d_cols_of = [client2_columns(0)]
         for j in range(HALF_UNITS, UNITS):
             quantise_unit(1, j, grouped_of[j])
-        for j in range(HALF_UNITS, UNITS):
-            noisy_rows(j, multiplier)
         fuse_columns(0, d_cols_of[0])
         d_cols_of.append(client2_columns(1))
         for t in range(HALF_TILES):
             store_rows(t, d_cols_of[0], nc.scalar.copy)
+        for j in range(HALF_UNITS, UNITS):
+            noisy_rows(j, multiplier)
         for j in range(HALF_UNITS, UNITS):
             mask_rows(j)
         for t in range(HALF_TILES, ROW_TILES):

@@ -55,7 +55,8 @@ def tile_splitnn_pa_kernel(
         x_sb = [[data.tile([P, F], BF16, name="x%d_%d" % (c, t)) for t in range(ROW_TILES)] for c in range(2)]
         noise_sb = data.tile([P, ROW_TILES, H], BF16)
         rows_sb = [data.tile([P, UNIT_TILES, H], F32, name="rows%d" % j) for j in range(UNITS)]
-        norms = const.tile([P, ROW_TILES], F32)
+        signed_norms = const.tile([P, 2, ROW_TILES], F32)
+        norms = signed_norms[:, 0, :]
         x_codes = [
             [data.tile([P, PASSES, MOVING], U32, name="x_codes%d_%d" % (c, n), align_bytes=64) for n in range(HALVES)]
             for c in range(2)
@@ -178,24 +179,18 @@ def tile_splitnn_pa_kernel(
                 )
 
         def noise_multiplier():
-            part_max = const.tile([P, 1], F32)
-            nc.vector.tensor_reduce(out=part_max[:], in_=norms[:], axis=AX.X, op=ALU.max)
-            part_min = const.tile([P, 1], F32)
-            nc.vector.tensor_reduce(out=part_min[:], in_=norms[:], axis=AX.X, op=ALU.min)
-            repeated = const.tile([P, 2, P], F32)
-            nc.vector.tensor_copy(out=repeated[:, 0, :], in_=part_max[:, 0:1].to_broadcast([P, P]))
-            nc.vector.tensor_copy(out=repeated[:, 1, :], in_=part_min[:, 0:1].to_broadcast([P, P]))
+            nc.vector.tensor_scalar_mul(out=signed_norms[:, 1, :], in0=signed_norms[:, 0, :], scalar1=-1.0)
+            part = const.tile([P, 2], F32)
+            nc.vector.tensor_reduce(out=part[:], in_=signed_norms[:], axis=AX.X, op=ALU.max)
             across = psum.tile([P, 2, P], F32, tag="bank")
-            nc.tensor.transpose(across[:, 0, :], repeated[:, 0, :], ident[:])
-            nc.tensor.transpose(across[:, 1, :], repeated[:, 1, :], ident[:])
-            all_max = const.tile([P, 1], F32)
-            nc.vector.tensor_reduce(out=all_max[:], in_=across[:, 0, :], axis=AX.X, op=ALU.max)
-            all_min = const.tile([P, 1], F32)
-            nc.vector.tensor_reduce(out=all_min[:], in_=across[:, 1, :], axis=AX.X, op=ALU.min)
+            for e in range(2):
+                nc.tensor.transpose(across[:, e, :], part[:, e : e + 1].to_broadcast([P, P]), ident[:])
+            both = const.tile([P, 2], F32)
+            nc.vector.tensor_reduce(out=both[:], in_=across[:], axis=AX.X, op=ALU.max)
             multiplier = const.tile([P, 1], F32)
             nc.vector.tensor_scalar(
-                out=multiplier[:], in0=all_max[:], scalar1=all_min[:, 0:1], scalar2=INV_EPS,
-                op0=ALU.subtract, op1=ALU.mult,
+                out=multiplier[:], in0=both[:, 0:1], scalar1=both[:, 1:2], scalar2=INV_EPS,
+                op0=ALU.add, op1=ALU.mult,
             )
             return multiplier
 

@@ -90,9 +90,8 @@ def tile_splitnn_pa_kernel(
                 out=w_words[c][:].bitcast(I32), in_=words.bitcast(I32).rearrange("g p b -> p g b")
             )
 
-        load_x(0, range(HALF_TILES))
+        load_x(0, range(ROW_TILES))
         load_weight(0, W1_words, W1_scales)
-        load_x(0, range(HALF_TILES, ROW_TILES))
         load_weight(1, W2_words, W2_scales)
         load_x(1, range(HALF_TILES))
         nc.sync.dma_start(out=noise_sb[:], in_=noise_rows)

@@ -52,7 +52,7 @@ def tile_splitnn_pa_kernel(
 
         w_words = [const.tile([P, PASSES, 2 * H], U8, name="w_words%d" % c, align_bytes=64) for c in range(2)]
         w_planes = [const.tile([P, PASSES, H], U8, name="w_planes%d" % c, align_bytes=64) for c in range(2)]
-        x_sb = [[data.tile([P, F], BF16, name="x%d_%d" % (c, t)) for t in range(ROW_TILES)] for c in range(2)]
+        x_sb = [{}, {}]
         noise_sb = data.tile([P, ROW_TILES, H], BF16)
         rows_sb = [data.tile([P, UNIT_TILES, H], F32, name="rows%d" % j) for j in range(UNITS)]
         signed_norms = const.tile([P, 2, ROW_TILES], F32)
@@ -66,39 +66,44 @@ def tile_splitnn_pa_kernel(
             for c in range(2)
         ]
 
-        for c in range(2):
-            nc.vector.memset(w_planes[c][:].bitcast(I32), 0)
         vec_rows = const.tile([P, 3, H], BF16)
-        nc.vector.memset(vec_rows[:], 0.0)
-        ones = const.tile([P, P], BF16)
-        nc.vector.memset(ones[:], 1.0)
+        nc.vector.memset(vec_rows[:].rearrange("p v h -> p (v h)").bitcast(I32), 0)
         table_warmer = const.tile([P, 1], F32)
         nc.vector.memset(table_warmer[:], 0.0)
+        for c in range(2):
+            nc.vector.memset(w_planes[c][:].bitcast(I32), 0)
+        ones = const.tile([P, P], BF16)
+        nc.vector.memset(ones[:], 1.0)
         ident = const.tile([P, P], F32)
         make_identity(nc, ident[:])
 
-        def load_x(c, tiles):
-            for t in tiles:
-                nc.sync.dma_start(out=x_sb[c][t][:], in_=x_rows[c][:, t, :])
+        def load_x(c, first, end):
+            rows = data.tile([P, end - first, F], BF16, name="x%d_%d" % (c, first))
+            nc.sync.dma_start(out=rows[:], in_=x_rows[c][:, first:end, :])
+            for t in range(first, end):
+                x_sb[c][t] = rows[:, t - first, :]
 
         def load_weight(c, words, scales):
+            nc.sync.dma_start(
+                out=w_words[c][:].bitcast(I32), in_=words.bitcast(I32).rearrange("g p b -> p g b")
+            )
             plane_words = w_planes[c][:].bitcast(I32)
             scale_rows = scales.bitcast(I32).rearrange("g (q l) n -> l q g n", l=4)
             for l in range(4):
                 nc.sync.dma_start(out=plane_words[l:P:32, :, :], in_=scale_rows[l])
-            nc.sync.dma_start(
-                out=w_words[c][:].bitcast(I32), in_=words.bitcast(I32).rearrange("g p b -> p g b")
-            )
 
-        load_x(0, range(ROW_TILES))
-        load_weight(0, W1_words, W1_scales)
-        load_weight(1, W2_words, W2_scales)
-        load_x(1, range(HALF_TILES))
-        nc.sync.dma_start(out=noise_sb[:], in_=noise_rows)
-        load_x(1, range(HALF_TILES, ROW_TILES))
+        load_x(0, 0, 1)
+        load_x(0, 1, 2)
         for v, vec in enumerate((b1, b2, rr_uniform)):
-            nc.scalar.dma_start(out=vec_rows[0:1, v, :], in_=vec.unsqueeze(0))
-
+            nc.sync.dma_start(out=vec_rows[0:1, v, :], in_=vec.unsqueeze(0))
+        for first in range(UNIT_TILES, ROW_TILES, UNIT_TILES):
+            load_x(0, first, first + UNIT_TILES)
+        load_weight(0, W1_words, W1_scales)
+        for first in range(0, HALF_TILES, UNIT_TILES):
+            load_x(1, first, first + UNIT_TILES)
+        load_weight(1, W2_words, W2_scales)
+        load_x(1, HALF_TILES, ROW_TILES)
+        nc.sync.dma_start(out=noise_sb[:], in_=noise_rows)
         nc.scalar.activation(out=table_warmer[:], in_=table_warmer[:], func=ACT.Abs)
 
         b1_all = const.tile([P, H], F32)
@@ -125,10 +130,10 @@ def tile_splitnn_pa_kernel(
                     )
             nc.scalar.copy(out=cols[:], in_=cols_ps[:])
 
-        def transpose_unit(c, j):
+        def transpose_unit(c, j, copies):
             grouped = stage.tile([P, PASSES, UNIT_TILES, P, PACK], BF16, align_bytes=64, tag="grouped")
             for i in range(UNIT_TILES):
-                x_words = x_sb[c][j * UNIT_TILES + i][:].bitcast(F32)
+                x_words = x_sb[c][j * UNIT_TILES + i].bitcast(F32)
                 xt = psum.tile([P, PASSES * WORD_HALVES, P], F32, tag="bank")
                 for g in range(PASSES):
                     first = g * K_PASS // 2
@@ -138,8 +143,7 @@ def tile_splitnn_pa_kernel(
                             x_words[:, first + u : first + K_PASS // 2 : WORD_HALVES],
                             ident[:],
                         )
-                copy_out = nc.vector.tensor_copy if (c == 0 and i % 2 == 1 and j < HALF_UNITS) else nc.scalar.copy
-                copy_out(
+                copies[i](
                     out=grouped[:, :, i, :, :].bitcast(F32),
                     in_=xt[:].rearrange("p (g u) r -> p g r u", u=WORD_HALVES),
                 )
@@ -172,10 +176,16 @@ def tile_splitnn_pa_kernel(
                         stop=(g == PASSES - 1),
                     )
                 nc.vector.tensor_tensor(out=rows_sb[j][:, i, :], in0=acc[:], in1=b1_all[:], op=ALU.add)
-                absolute = stage.tile([P, H], BF16, tag="absolute")
-                nc.scalar.activation(
-                    out=absolute[:], in_=rows_sb[j][:, i, :], func=ACT.Abs, accum_out=norms[:, t : t + 1]
-                )
+                if t == ROW_TILES - 1:
+                    nc.vector.tensor_reduce(
+                        out=norms[:, t : t + 1], in_=rows_sb[j][:, i, :], axis=AX.X, op=ALU.add,
+                        apply_absolute_value=True,
+                    )
+                else:
+                    absolute = stage.tile([P, H], BF16, tag="absolute")
+                    nc.scalar.activation(
+                        out=absolute[:], in_=rows_sb[j][:, i, :], func=ACT.Abs, accum_out=norms[:, t : t + 1]
+                    )
 
         def noise_multiplier():
             nc.vector.tensor_scalar_mul(out=signed_norms[:, 1, :], in0=signed_norms[:, 0, :], scalar1=-1.0)
@@ -256,26 +266,28 @@ def tile_splitnn_pa_kernel(
             copy_out(out=out_sb[:], in_=out_ps[:].rearrange("p a m -> p (a m)"))
             nc.sync.dma_start(out=out_rows[:, t, :], in_=out_sb[:])
 
-        for j in range(LAG):
-            quantise_unit(0, j, transpose_unit(0, j))
+        by_scalar = [nc.scalar.copy] * UNIT_TILES
+        shared = [nc.scalar.copy, nc.vector.tensor_copy]
+        for j in range(UNITS):
+            grouped = transpose_unit(0, j, shared if j < HALF_UNITS else by_scalar)
+            if j + 1 < UNITS:
+                quantise_unit(0, j, grouped)
             if j == 0:
                 spread_vectors()
         for j in range(UNITS):
-            if j + LAG < UNITS:
-                grouped = transpose_unit(0, j + LAG)
             client1_rows(j)
-            if j + LAG < UNITS:
-                quantise_unit(0, j + LAG, grouped)
+            if j == 0:
+                quantise_unit(0, UNITS - 1, grouped)
 
         column_vectors()
-        grouped_of = [transpose_unit(1, j) for j in range(HALF_UNITS)]
+        grouped_of = [transpose_unit(1, j, by_scalar) for j in range(HALF_UNITS)]
         multiplier = noise_multiplier()
         for j in range(HALF_UNITS):
             quantise_unit(1, j, grouped_of[j])
         noisy_rows(0, multiplier)
-        grouped_of.append(transpose_unit(1, 2))
+        grouped_of.append(transpose_unit(1, 2, by_scalar))
         noisy_rows(1, multiplier)
-        grouped_of.append(transpose_unit(1, 3))
+        grouped_of.append(transpose_unit(1, 3, by_scalar))
         nc.vector.tensor_single_scalar(out=keep_cols[:], in_=cols[:, 1, :], scalar=P_KEEP, op=ALU.is_lt)
         d_cols_of = [client2_columns(0)]
         for j in range(HALF_UNITS, UNITS):

@@ -223,11 +223,11 @@ def tile_splitnn_pa_kernel(
             return d_cols
 
         def noisy_rows(j, multiplier):
-            tiles = slice(j * UNIT_TILES, (j + 1) * UNIT_TILES)
-            nc.vector.scalar_tensor_tensor(
-                out=rows_sb[j][:], in0=noise_sb[:, tiles, :], scalar=multiplier[:, 0:1], in1=rows_sb[j][:],
-                op0=ALU.mult, op1=ALU.add,
-            )
+            for i in range(UNIT_TILES):
+                nc.vector.scalar_tensor_tensor(
+                    out=rows_sb[j][:, i, :], in0=noise_sb[:, j * UNIT_TILES + i, :], scalar=multiplier[:, 0:1],
+                    in1=rows_sb[j][:, i, :], op0=ALU.mult, op1=ALU.add,
+                )
 
         def fuse_columns(half, d_cols):
             for a in range(H_SLICES):
@@ -242,11 +242,9 @@ def tile_splitnn_pa_kernel(
                     in1=d_cols[:, a, :], op0=ALU.mult, op1=ALU.min,
                 )
 
-        def mask_rows(j):
-            nc.vector.tensor_tensor(
-                out=rows_sb[j][:], in0=rows_sb[j][:],
-                in1=keep_all[:].unsqueeze(1).to_broadcast([P, UNIT_TILES, H]), op=ALU.mult,
-            )
+        def mask_rows(j, engine):
+            for i in range(UNIT_TILES):
+                engine.tensor_tensor(out=rows_sb[j][:, i, :], in0=rows_sb[j][:, i, :], in1=keep_all[:], op=ALU.mult)
 
         def finish_rows(t, d_cols):
             rows = slice((t % HALF_TILES) * P, (t % HALF_TILES + 1) * P)
@@ -292,13 +290,14 @@ def tile_splitnn_pa_kernel(
         d_cols_of = [client2_columns(0)]
         for j in range(HALF_UNITS, UNITS):
             quantise_unit(1, j, grouped_of[j])
+        noisy_rows(UNITS - 1, multiplier)
+        mask_rows(UNITS - 1, nc.gpsimd)
         fuse_columns(0, d_cols_of[0])
         d_cols_of.append(client2_columns(1))
         for t in range(HALF_TILES):
             store_rows(t, d_cols_of[0], nc.scalar.copy)
-        for j in range(HALF_UNITS, UNITS):
+        for j in range(HALF_UNITS, UNITS - 1):
             noisy_rows(j, multiplier)
-        for j in range(HALF_UNITS, UNITS):
-            mask_rows(j)
+            mask_rows(j, nc.vector)
         for t in range(HALF_TILES, ROW_TILES):
             finish_rows(t, d_cols_of[1])

@@ -29,6 +29,7 @@ HALVES = ROW_TILES // HALF_TILES
 LAG = HALF_UNITS
 H_SLICES = H // P
 WORD_HALVES = 2
+WARM_MATMULS = 3
 INV_EPS = 30.0 / 4.0
 P_KEEP = 0.95
 
@@ -57,6 +58,7 @@ def tile_splitnn_pa_kernel(
         rows_sb = [data.tile([P, UNIT_TILES, H], F32, name="rows%d" % j) for j in range(UNITS)]
         signed_norms = const.tile([P, 2, ROW_TILES], F32)
         norms = signed_norms[:, 0, :]
+        scaled_noise = data.tile([P, H], F32)
         x_codes = [
             [data.tile([P, PASSES, MOVING], U32, name="x_codes%d_%d" % (c, n), align_bytes=64) for n in range(HALVES)]
             for c in range(2)
@@ -66,6 +68,8 @@ def tile_splitnn_pa_kernel(
             for c in range(2)
         ]
 
+        zeros = const.tile([P, H], BF16)
+        nc.gpsimd.memset(zeros[:].bitcast(F32), 0.0)
         vec_rows = const.tile([P, 3, H], BF16)
         nc.vector.memset(vec_rows[:].rearrange("p v h -> p (v h)").bitcast(I32), 0)
         table_warmer = const.tile([P, 1], F32)
@@ -222,8 +226,11 @@ def tile_splitnn_pa_kernel(
                 )
             return d_cols
 
-        def noisy_rows(j, multiplier):
-            for i in range(UNIT_TILES):
+        def scale_noise(t, multiplier):
+            nc.scalar.activation(out=scaled_noise[:], in_=noise_sb[:, t, :], func=ACT.Copy, scale=multiplier[:, 0:1])
+
+        def noisy_rows(j, multiplier, tiles=range(UNIT_TILES)):
+            for i in tiles:
                 nc.vector.scalar_tensor_tensor(
                     out=rows_sb[j][:, i, :], in0=noise_sb[:, j * UNIT_TILES + i, :], scalar=multiplier[:, 0:1],
                     in1=rows_sb[j][:, i, :], op0=ALU.mult, op1=ALU.add,
@@ -234,9 +241,14 @@ def tile_splitnn_pa_kernel(
                 c_cols = psum.tile([P, HALF_TILES, P], F32, tag="bank")
                 for i in range(HALF_TILES):
                     t = half * HALF_TILES + i
-                    nc.tensor.transpose(
-                        c_cols[:, i, :], rows_sb[t // UNIT_TILES][:, t % UNIT_TILES, a * P : (a + 1) * P], ident[:]
-                    )
+                    rows = [rows_sb[t // UNIT_TILES][:, t % UNIT_TILES, :]]
+                    if t == HALF_TILES - 1:
+                        rows.append(scaled_noise[:])
+                    for n, term in enumerate(rows):
+                        nc.tensor.matmul(
+                            out=c_cols[:, i, :], lhsT=term[:, a * P : (a + 1) * P], rhs=ident[:], is_transpose=True,
+                            start=(n == 0), stop=(n == len(rows) - 1),
+                        )
                 nc.vector.scalar_tensor_tensor(
                     out=d_cols[:, a, :], in0=c_cols[:].rearrange("p i r -> p (i r)"), scalar=keep_cols[:, a : a + 1],
                     in1=d_cols[:, a, :], op0=ALU.mult, op1=ALU.min,
@@ -264,6 +276,9 @@ def tile_splitnn_pa_kernel(
             copy_out(out=out_sb[:], in_=out_ps[:].rearrange("p a m -> p (a m)"))
             nc.sync.dma_start(out=out_rows[:, t, :], in_=out_sb[:])
 
+        warm_ps = psum.tile([P, H], F32, tag="bank")
+        for n in range(WARM_MATMULS):
+            nc.tensor.matmul(out=warm_ps[:], lhsT=zeros[:, :P], rhs=zeros[:], start=True, stop=True)
         by_scalar = [nc.scalar.copy] * UNIT_TILES
         shared = [nc.scalar.copy, nc.vector.tensor_copy]
         for j in range(UNITS):
@@ -284,7 +299,8 @@ def tile_splitnn_pa_kernel(
             quantise_unit(1, j, grouped_of[j])
         noisy_rows(0, multiplier)
         grouped_of.append(transpose_unit(1, 2, by_scalar))
-        noisy_rows(1, multiplier)
+        scale_noise(HALF_TILES - 1, multiplier)
+        noisy_rows(1, multiplier, range(1))
         grouped_of.append(transpose_unit(1, 3, by_scalar))
         nc.vector.tensor_single_scalar(out=keep_cols[:], in_=cols[:, 1, :], scalar=P_KEEP, op=ALU.is_lt)
         d_cols_of = [client2_columns(0)]

@@ -56,9 +56,7 @@ def tile_splitnn_pa_kernel(
         x_sb = [{}, {}]
         noise_sb = data.tile([P, ROW_TILES, H], BF16)
         rows_sb = [data.tile([P, UNIT_TILES, H], F32, name="rows%d" % j) for j in range(UNITS)]
-        signed_norms = const.tile([P, 2, ROW_TILES], F32)
-        norms = signed_norms[:, 0, :]
-        scaled_noise = data.tile([P, H], F32)
+        norms = const.tile([P, ROW_TILES], F32)
         x_codes = [
             [data.tile([P, PASSES, MOVING], U32, name="x_codes%d_%d" % (c, n), align_bytes=64) for n in range(HALVES)]
             for c in range(2)
@@ -101,8 +99,9 @@ def tile_splitnn_pa_kernel(
         for v, vec in enumerate((b1, b2, rr_uniform)):
             nc.sync.dma_start(out=vec_rows[0:1, v, :], in_=vec.unsqueeze(0))
         for first in range(UNIT_TILES, ROW_TILES, UNIT_TILES):
+            if first == ROW_TILES - UNIT_TILES:
+                load_weight(0, W1_words, W1_scales)
             load_x(0, first, first + UNIT_TILES)
-        load_weight(0, W1_words, W1_scales)
         for first in range(0, HALF_TILES, UNIT_TILES):
             load_x(1, first, first + UNIT_TILES)
         load_weight(1, W2_words, W2_scales)
@@ -134,33 +133,45 @@ def tile_splitnn_pa_kernel(
                     )
             nc.scalar.copy(out=cols[:], in_=cols_ps[:])
 
-        def transpose_unit(c, j, copies):
-            grouped = stage.tile([P, PASSES, UNIT_TILES, P, PACK], BF16, align_bytes=64, tag="grouped")
-            for i in range(UNIT_TILES):
-                x_words = x_sb[c][j * UNIT_TILES + i].bitcast(F32)
-                xt = psum.tile([P, PASSES * WORD_HALVES, P], F32, tag="bank")
-                for g in range(PASSES):
-                    first = g * K_PASS // 2
-                    for u in range(WORD_HALVES):
-                        nc.tensor.transpose(
-                            xt[:, g * WORD_HALVES + u, :],
-                            x_words[:, first + u : first + K_PASS // 2 : WORD_HALVES],
-                            ident[:],
-                        )
-                copies[i](
-                    out=grouped[:, :, i, :, :].bitcast(F32),
-                    in_=xt[:].rearrange("p (g u) r -> p g r u", u=WORD_HALVES),
-                )
-            return grouped
+        turned, grouped = {}, {}
+        extremes = (ALU.max, ALU.min)
 
-        def quantise_unit(c, j, grouped):
+        def transpose_tile(c, t):
+            x_words = x_sb[c][t].bitcast(F32)
+            turned[c, t] = psum.tile([P, PASSES * WORD_HALVES, P], F32, tag="bank", name="turned")
+            for g in range(PASSES):
+                first = g * K_PASS // 2
+                for u in range(WORD_HALVES):
+                    nc.tensor.transpose(
+                        turned[c, t][:, g * WORD_HALVES + u, :],
+                        x_words[:, first + u : first + K_PASS // 2 : WORD_HALVES],
+                        ident[:],
+                    )
+
+        def group_tile(c, t, copy_out):
+            j, i = divmod(t, UNIT_TILES)
+            if (c, j) not in grouped:
+                grouped[c, j] = stage.tile(
+                    [P, PASSES, UNIT_TILES, P, PACK], BF16, align_bytes=64, tag="grouped", name="grouped"
+                )
+            copy_out(
+                out=grouped[c, j][:, :, i, :, :].bitcast(F32),
+                in_=turned[c, t][:].rearrange("p (g u) r -> p g r u", u=WORD_HALVES),
+            )
+
+        def transpose_unit(c, j, copies):
+            for i in range(UNIT_TILES):
+                transpose_tile(c, j * UNIT_TILES + i)
+                group_tile(c, j * UNIT_TILES + i, copies[i])
+
+        def quantise_unit(c, j):
             half = j // HALF_UNITS
             rows = slice((j % HALF_UNITS) * UNIT_TILES * P, (j % HALF_UNITS + 1) * UNIT_TILES * P)
             for g in range(PASSES):
                 nc.vector.quantize_mx(
                     out=x_codes[c][half][:, g, rows].bitcast(FP8X4),
                     scales=x_planes[c][half][:, g, rows],
-                    in_=grouped[:, g, :, :, :].rearrange("p i r s -> p (i r s)"),
+                    in_=grouped[c, j][:, g, :, :, :].rearrange("p i r s -> p (i r s)"),
                 )
 
         def client1_rows(j):
@@ -180,30 +191,34 @@ def tile_splitnn_pa_kernel(
                         stop=(g == PASSES - 1),
                     )
                 nc.vector.tensor_tensor(out=rows_sb[j][:, i, :], in0=acc[:], in1=b1_all[:], op=ALU.add)
-                if t == ROW_TILES - 1:
-                    nc.vector.tensor_reduce(
-                        out=norms[:, t : t + 1], in_=rows_sb[j][:, i, :], axis=AX.X, op=ALU.add,
-                        apply_absolute_value=True,
-                    )
-                else:
-                    absolute = stage.tile([P, H], BF16, tag="absolute")
-                    nc.scalar.activation(
-                        out=absolute[:], in_=rows_sb[j][:, i, :], func=ACT.Abs, accum_out=norms[:, t : t + 1]
-                    )
 
-        def noise_multiplier():
-            nc.vector.tensor_scalar_mul(out=signed_norms[:, 1, :], in0=signed_norms[:, 0, :], scalar1=-1.0)
+        def row_norms(t):
+            rows = rows_sb[t // UNIT_TILES][:, t % UNIT_TILES, :]
+            if t == ROW_TILES - 1:
+                nc.vector.tensor_reduce(
+                    out=norms[:, t : t + 1], in_=rows, axis=AX.X, op=ALU.add, apply_absolute_value=True
+                )
+            else:
+                absolute = stage.tile([P, H], BF16, tag="absolute")
+                nc.scalar.activation(out=absolute[:], in_=rows, func=ACT.Abs, accum_out=norms[:, t : t + 1])
+
+        def extremes_across():
             part = const.tile([P, 2], F32)
-            nc.vector.tensor_reduce(out=part[:], in_=signed_norms[:], axis=AX.X, op=ALU.max)
+            for e, extreme in enumerate(extremes):
+                nc.vector.tensor_reduce(out=part[:, e : e + 1], in_=norms[:], axis=AX.X, op=extreme)
             across = psum.tile([P, 2, P], F32, tag="bank")
             for e in range(2):
                 nc.tensor.transpose(across[:, e, :], part[:, e : e + 1].to_broadcast([P, P]), ident[:])
+            return across
+
+        def noise_multiplier(across):
             both = const.tile([P, 2], F32)
-            nc.vector.tensor_reduce(out=both[:], in_=across[:], axis=AX.X, op=ALU.max)
+            for e, extreme in enumerate(extremes):
+                nc.vector.tensor_reduce(out=both[:, e : e + 1], in_=across[:, e, :], axis=AX.X, op=extreme)
             multiplier = const.tile([P, 1], F32)
             nc.vector.tensor_scalar(
                 out=multiplier[:], in0=both[:, 0:1], scalar1=both[:, 1:2], scalar2=INV_EPS,
-                op0=ALU.add, op1=ALU.mult,
+                op0=ALU.subtract, op1=ALU.mult,
             )
             return multiplier
 
@@ -226,37 +241,28 @@ def tile_splitnn_pa_kernel(
                 )
             return d_cols
 
-        def scale_noise(t, multiplier):
-            nc.scalar.activation(out=scaled_noise[:], in_=noise_sb[:, t, :], func=ACT.Copy, scale=multiplier[:, 0:1])
-
-        def noisy_rows(j, multiplier, tiles=range(UNIT_TILES)):
-            for i in tiles:
-                nc.vector.scalar_tensor_tensor(
-                    out=rows_sb[j][:, i, :], in0=noise_sb[:, j * UNIT_TILES + i, :], scalar=multiplier[:, 0:1],
-                    in1=rows_sb[j][:, i, :], op0=ALU.mult, op1=ALU.add,
-                )
+        def noisy_rows(t, multiplier):
+            rows = rows_sb[t // UNIT_TILES][:, t % UNIT_TILES, :]
+            nc.vector.scalar_tensor_tensor(
+                out=rows, in0=noise_sb[:, t, :], scalar=multiplier[:, 0:1], in1=rows, op0=ALU.mult, op1=ALU.add
+            )
 
         def fuse_columns(half, d_cols):
             for a in range(H_SLICES):
                 c_cols = psum.tile([P, HALF_TILES, P], F32, tag="bank")
                 for i in range(HALF_TILES):
                     t = half * HALF_TILES + i
-                    rows = [rows_sb[t // UNIT_TILES][:, t % UNIT_TILES, :]]
-                    if t == HALF_TILES - 1:
-                        rows.append(scaled_noise[:])
-                    for n, term in enumerate(rows):
-                        nc.tensor.matmul(
-                            out=c_cols[:, i, :], lhsT=term[:, a * P : (a + 1) * P], rhs=ident[:], is_transpose=True,
-                            start=(n == 0), stop=(n == len(rows) - 1),
-                        )
+                    nc.tensor.transpose(
+                        c_cols[:, i, :], rows_sb[t // UNIT_TILES][:, t % UNIT_TILES, a * P : (a + 1) * P], ident[:]
+                    )
                 nc.vector.scalar_tensor_tensor(
                     out=d_cols[:, a, :], in0=c_cols[:].rearrange("p i r -> p (i r)"), scalar=keep_cols[:, a : a + 1],
                     in1=d_cols[:, a, :], op0=ALU.mult, op1=ALU.min,
                 )
 
-        def mask_rows(j, engine):
-            for i in range(UNIT_TILES):
-                engine.tensor_tensor(out=rows_sb[j][:, i, :], in0=rows_sb[j][:, i, :], in1=keep_all[:], op=ALU.mult)
+        def mask_rows(t, engine):
+            rows = rows_sb[t // UNIT_TILES][:, t % UNIT_TILES, :]
+            engine.tensor_tensor(out=rows, in0=rows, in1=keep_all[:], op=ALU.mult)
 
         def finish_rows(t, d_cols):
             rows = slice((t % HALF_TILES) * P, (t % HALF_TILES + 1) * P)
@@ -281,39 +287,54 @@ def tile_splitnn_pa_kernel(
             nc.tensor.matmul(out=warm_ps[:], lhsT=zeros[:, :P], rhs=zeros[:], start=True, stop=True)
         by_scalar = [nc.scalar.copy] * UNIT_TILES
         shared = [nc.scalar.copy, nc.vector.tensor_copy]
-        for j in range(UNITS):
-            grouped = transpose_unit(0, j, shared if j < HALF_UNITS else by_scalar)
-            if j + 1 < UNITS:
-                quantise_unit(0, j, grouped)
-            if j == 0:
-                spread_vectors()
-        for j in range(UNITS):
+        transpose_unit(0, 0, shared)
+        quantise_unit(0, 0)
+        spread_vectors()
+        transpose_unit(0, 1, by_scalar)
+        quantise_unit(0, 1)
+        transpose_unit(0, 2, by_scalar)
+        client1_rows(0)
+        quantise_unit(0, 2)
+        row_norms(0)
+        transpose_unit(0, 3, by_scalar)
+        row_norms(1)
+        for j in range(1, UNITS):
             client1_rows(j)
-            if j == 0:
-                quantise_unit(0, UNITS - 1, grouped)
+            if j == 1:
+                quantise_unit(0, UNITS - 1)
+            for t in range(j * UNIT_TILES, (j + 1) * UNIT_TILES):
+                row_norms(t)
 
         column_vectors()
-        grouped_of = [transpose_unit(1, j, by_scalar) for j in range(HALF_UNITS)]
-        multiplier = noise_multiplier()
+        for t in range(HALF_TILES):
+            transpose_tile(1, t)
+        for t in range(1, HALF_TILES):
+            group_tile(1, t, nc.scalar.copy)
+        across = extremes_across()
+        group_tile(1, 0, nc.vector.tensor_copy)
+        multiplier = noise_multiplier(across)
         for j in range(HALF_UNITS):
-            quantise_unit(1, j, grouped_of[j])
-        noisy_rows(0, multiplier)
-        grouped_of.append(transpose_unit(1, 2, by_scalar))
-        scale_noise(HALF_TILES - 1, multiplier)
-        noisy_rows(1, multiplier, range(1))
-        grouped_of.append(transpose_unit(1, 3, by_scalar))
+            quantise_unit(1, j)
+        for j in range(HALF_UNITS, UNITS):
+            transpose_unit(1, j, by_scalar)
+        for t in range(HALF_TILES):
+            noisy_rows(t, multiplier)
         nc.vector.tensor_single_scalar(out=keep_cols[:], in_=cols[:, 1, :], scalar=P_KEEP, op=ALU.is_lt)
         d_cols_of = [client2_columns(0)]
         for j in range(HALF_UNITS, UNITS):
-            quantise_unit(1, j, grouped_of[j])
-        noisy_rows(UNITS - 1, multiplier)
-        mask_rows(UNITS - 1, nc.gpsimd)
+            quantise_unit(1, j)
+        by_gpsimd = (ROW_TILES - 1, ROW_TILES - 3)
+        by_vector = (ROW_TILES - 4, ROW_TILES - 2)
+        noisy_rows(by_gpsimd[0], multiplier)
+        mask_rows(by_gpsimd[0], nc.gpsimd)
         fuse_columns(0, d_cols_of[0])
         d_cols_of.append(client2_columns(1))
         for t in range(HALF_TILES):
             store_rows(t, d_cols_of[0], nc.scalar.copy)
-        for j in range(HALF_UNITS, UNITS - 1):
-            noisy_rows(j, multiplier)
-            mask_rows(j, nc.vector)
-        for t in range(HALF_TILES, ROW_TILES):
+        for t in by_vector:
+            noisy_rows(t, multiplier)
+            mask_rows(t, nc.vector)
+        noisy_rows(by_gpsimd[1], multiplier)
+        mask_rows(by_gpsimd[1], nc.gpsimd)
+        for t in (by_vector[0], by_gpsimd[0], by_vector[1], by_gpsimd[1]):
             finish_rows(t, d_cols_of[1])

@@ -68,10 +68,13 @@ def tile_splitnn_pa_kernel(
 
         zeros = const.tile([P, H], BF16)
         nc.gpsimd.memset(zeros[:].bitcast(F32), 0.0)
-        vec_rows = const.tile([P, 3, H], BF16)
-        nc.vector.memset(vec_rows[:].rearrange("p v h -> p (v h)").bitcast(I32), 0)
+        first_rows = const.tile([P, 2, H], BF16)
+        b2_row = const.tile([P, H], BF16)
+        b1_row, u_row = first_rows[:, 0, :], first_rows[:, 1, :]
+        nc.vector.memset(first_rows[:].rearrange("p v h -> p (v h)").bitcast(I32), 0)
         table_warmer = const.tile([P, 1], F32)
         nc.vector.memset(table_warmer[:], 0.0)
+        nc.vector.memset(b2_row[:].bitcast(I32), 0)
         for c in range(2):
             nc.vector.memset(w_planes[c][:].bitcast(I32), 0)
         ones = const.tile([P, P], BF16)
@@ -96,12 +99,13 @@ def tile_splitnn_pa_kernel(
 
         load_x(0, 0, 1)
         load_x(0, 1, 2)
-        for v, vec in enumerate((b1, b2, rr_uniform)):
-            nc.sync.dma_start(out=vec_rows[0:1, v, :], in_=vec.unsqueeze(0))
+        nc.sync.dma_start(out=b1_row[0:1, :], in_=b1.unsqueeze(0))
+        nc.sync.dma_start(out=u_row[0:1, :], in_=rr_uniform.unsqueeze(0))
         for first in range(UNIT_TILES, ROW_TILES, UNIT_TILES):
             if first == ROW_TILES - UNIT_TILES:
                 load_weight(0, W1_words, W1_scales)
             load_x(0, first, first + UNIT_TILES)
+        nc.sync.dma_start(out=b2_row[0:1, :], in_=b2.unsqueeze(0))
         for first in range(0, HALF_TILES, UNIT_TILES):
             load_x(1, first, first + UNIT_TILES)
         load_weight(1, W2_words, W2_scales)
@@ -117,18 +121,18 @@ def tile_splitnn_pa_kernel(
 
         def spread_vectors():
             spread_ps = psum.tile([P, H], F32, tag="bank")
-            nc.tensor.matmul(out=spread_ps[:], lhsT=ones[:], rhs=vec_rows[:, 0, :], start=True, stop=True)
+            nc.tensor.matmul(out=spread_ps[:], lhsT=ones[:], rhs=b1_row, start=True, stop=True)
             nc.scalar.copy(out=b1_all[:], in_=spread_ps[:])
             u_ps = psum.tile([P, H], F32, tag="bank")
-            nc.tensor.matmul(out=u_ps[:], lhsT=ones[:], rhs=vec_rows[:, 2, :], start=True, stop=True)
+            nc.tensor.matmul(out=u_ps[:], lhsT=ones[:], rhs=u_row, start=True, stop=True)
             nc.vector.tensor_single_scalar(out=keep_all[:], in_=u_ps[:], scalar=P_KEEP, op=ALU.is_lt)
 
         def column_vectors():
             cols_ps = psum.tile([P, 2, H_SLICES], F32, tag="bank")
-            for v in range(2):
+            for v, row in enumerate((b2_row, u_row)):
                 for a in range(H_SLICES):
                     nc.tensor.matmul(
-                        out=cols_ps[:, v, a : a + 1], lhsT=vec_rows[:, v + 1, a * P : (a + 1) * P],
+                        out=cols_ps[:, v, a : a + 1], lhsT=row[:, a * P : (a + 1) * P],
                         rhs=ones[:, 0:1], start=True, stop=True,
                     )
             nc.scalar.copy(out=cols[:], in_=cols_ps[:])
@@ -193,14 +197,11 @@ def tile_splitnn_pa_kernel(
                 nc.vector.tensor_tensor(out=rows_sb[j][:, i, :], in0=acc[:], in1=b1_all[:], op=ALU.add)
 
         def row_norms(t):
-            rows = rows_sb[t // UNIT_TILES][:, t % UNIT_TILES, :]
-            if t == ROW_TILES - 1:
-                nc.vector.tensor_reduce(
-                    out=norms[:, t : t + 1], in_=rows, axis=AX.X, op=ALU.add, apply_absolute_value=True
-                )
-            else:
-                absolute = stage.tile([P, H], BF16, tag="absolute")
-                nc.scalar.activation(out=absolute[:], in_=rows, func=ACT.Abs, accum_out=norms[:, t : t + 1])
+            absolute = stage.tile([P, H], BF16, tag="absolute")
+            nc.scalar.activation(
+                out=absolute[:], in_=rows_sb[t // UNIT_TILES][:, t % UNIT_TILES, :], func=ACT.Abs,
+                accum_out=norms[:, t : t + 1],
+            )
 
         def extremes_across():
             part = const.tile([P, 2], F32)
@@ -308,13 +309,12 @@ def tile_splitnn_pa_kernel(
         column_vectors()
         for t in range(HALF_TILES):
             transpose_tile(1, t)
-        for t in range(1, HALF_TILES):
-            group_tile(1, t, nc.scalar.copy)
+        for t in range(HALF_TILES):
+            group_tile(1, t, nc.vector.tensor_copy if t < UNIT_TILES else nc.scalar.copy)
         across = extremes_across()
-        group_tile(1, 0, nc.vector.tensor_copy)
+        quantise_unit(1, 0)
         multiplier = noise_multiplier(across)
-        for j in range(HALF_UNITS):
-            quantise_unit(1, j)
+        quantise_unit(1, 1)
         for j in range(HALF_UNITS, UNITS):
             transpose_unit(1, j, by_scalar)
         for t in range(HALF_TILES):
@@ -333,6 +333,7 @@ def tile_splitnn_pa_kernel(
             store_rows(t, d_cols_of[0], nc.scalar.copy)
         for t in by_vector:
             noisy_rows(t, multiplier)
+        for t in by_vector:
             mask_rows(t, nc.vector)
         noisy_rows(by_gpsimd[1], multiplier)
         mask_rows(by_gpsimd[1], nc.gpsimd)

@@ -223,9 +223,8 @@ def tile_splitnn_pa_kernel(
             )
             return multiplier
 
-        def client2_columns(half):
-            d_cols = stage.tile([P, H_SLICES, MOVING], F32, tag="d_cols", bufs=2)
-            for a in range(H_SLICES):
+        def client2_columns(half, d_cols, slices):
+            for a in slices:
                 acc = psum.tile([P, MOVING], F32, tag="bank")
                 for g in range(PASSES):
                     nc.tensor.matmul_mx(
@@ -240,7 +239,6 @@ def tile_splitnn_pa_kernel(
                 nc.scalar.activation(
                     out=d_cols[:, a, :], in_=acc[:], func=ACT.Identity, bias=b2_cols[:, a : a + 1]
                 )
-            return d_cols
 
         def noisy_rows(t, multiplier):
             rows = rows_sb[t // UNIT_TILES][:, t % UNIT_TILES, :]
@@ -248,18 +246,21 @@ def tile_splitnn_pa_kernel(
                 out=rows, in0=noise_sb[:, t, :], scalar=multiplier[:, 0:1], in1=rows, op0=ALU.mult, op1=ALU.add
             )
 
-        def fuse_columns(half, d_cols):
-            for a in range(H_SLICES):
-                c_cols = psum.tile([P, HALF_TILES, P], F32, tag="bank")
-                for i in range(HALF_TILES):
-                    t = half * HALF_TILES + i
-                    nc.tensor.transpose(
-                        c_cols[:, i, :], rows_sb[t // UNIT_TILES][:, t % UNIT_TILES, a * P : (a + 1) * P], ident[:]
+        def fuse_columns(j, d_cols):
+            first = (j % HALF_UNITS) * UNIT_TILES
+            rows = slice(first * P, (first + UNIT_TILES) * P)
+            for pair in range(H_SLICES // 2):
+                c_cols = psum.tile([P, 2, UNIT_TILES, P], F32, tag="bank")
+                for s in range(2):
+                    a = 2 * pair + s
+                    for i in range(UNIT_TILES):
+                        nc.tensor.transpose(c_cols[:, s, i, :], rows_sb[j][:, i, a * P : (a + 1) * P], ident[:])
+                for s in range(2):
+                    a = 2 * pair + s
+                    nc.vector.scalar_tensor_tensor(
+                        out=d_cols[:, a, rows], in0=c_cols[:, s, :, :].rearrange("p i r -> p (i r)"),
+                        scalar=keep_cols[:, a : a + 1], in1=d_cols[:, a, rows], op0=ALU.mult, op1=ALU.min,
                     )
-                nc.vector.scalar_tensor_tensor(
-                    out=d_cols[:, a, :], in0=c_cols[:].rearrange("p i r -> p (i r)"), scalar=keep_cols[:, a : a + 1],
-                    in1=d_cols[:, a, :], op0=ALU.mult, op1=ALU.min,
-                )
 
         def mask_rows(t, engine):
             rows = rows_sb[t // UNIT_TILES][:, t % UNIT_TILES, :]
@@ -320,22 +321,24 @@ def tile_splitnn_pa_kernel(
         for t in range(HALF_TILES):
             noisy_rows(t, multiplier)
         nc.vector.tensor_single_scalar(out=keep_cols[:], in_=cols[:, 1, :], scalar=P_KEEP, op=ALU.is_lt)
-        d_cols_of = [client2_columns(0)]
+        d_cols_of = [
+            stage.tile([P, H_SLICES, MOVING], F32, tag="d_cols", name="d_cols", bufs=HALVES) for half in range(HALVES)
+        ]
+        client2_columns(0, d_cols_of[0], range(H_SLICES))
         for j in range(HALF_UNITS, UNITS):
             quantise_unit(1, j)
-        by_gpsimd = (ROW_TILES - 1, ROW_TILES - 3)
-        by_vector = (ROW_TILES - 4, ROW_TILES - 2)
-        noisy_rows(by_gpsimd[0], multiplier)
-        mask_rows(by_gpsimd[0], nc.gpsimd)
-        fuse_columns(0, d_cols_of[0])
-        d_cols_of.append(client2_columns(1))
-        for t in range(HALF_TILES):
-            store_rows(t, d_cols_of[0], nc.scalar.copy)
-        for t in by_vector:
+        noisy_rows(ROW_TILES - 1, multiplier)
+        mask_rows(ROW_TILES - 1, nc.gpsimd)
+        for j in range(HALF_UNITS):
+            fuse_columns(j, d_cols_of[0])
+        slices = range(H_SLICES)
+        for j in range(HALF_UNITS):
+            client2_columns(1, d_cols_of[1], slices[j * H_SLICES // HALF_UNITS : (j + 1) * H_SLICES // HALF_UNITS])
+            for t in range(j * UNIT_TILES, (j + 1) * UNIT_TILES):
+                store_rows(t, d_cols_of[0], nc.scalar.copy)
+        for t in range(HALF_TILES, ROW_TILES - 1):
             noisy_rows(t, multiplier)
-        for t in by_vector:
+        for t in range(HALF_TILES, ROW_TILES - 1):
             mask_rows(t, nc.vector)
-        noisy_rows(by_gpsimd[1], multiplier)
-        mask_rows(by_gpsimd[1], nc.gpsimd)
-        for t in (by_vector[0], by_gpsimd[0], by_vector[1], by_gpsimd[1]):
+        for t in range(HALF_TILES, ROW_TILES):
             finish_rows(t, d_cols_of[1])

@@ -30,6 +30,7 @@ LAG = HALF_UNITS
 H_SLICES = H // P
 WORD_HALVES = 2
 WARM_MATMULS = 3
+ALIGN = 256
 INV_EPS = 30.0 / 4.0
 P_KEEP = 0.95
 
@@ -51,25 +52,25 @@ def tile_splitnn_pa_kernel(
         psum = ctx.enter_context(tc.psum_pool(name="psum", bufs=8))
         ctx.enter_context(tc.manual_schedule())
 
-        w_words = [const.tile([P, PASSES, 2 * H], U8, name="w_words%d" % c, align_bytes=64) for c in range(2)]
-        w_planes = [const.tile([P, PASSES, H], U8, name="w_planes%d" % c, align_bytes=64) for c in range(2)]
+        w_words = [const.tile([P, PASSES, 2 * H], U8, name="w_words%d" % c, align_bytes=ALIGN) for c in range(2)]
+        w_planes = [const.tile([P, PASSES, H], U8, name="w_planes%d" % c, align_bytes=ALIGN) for c in range(2)]
         x_sb = [{}, {}]
-        noise_sb = data.tile([P, ROW_TILES, H], BF16)
-        rows_sb = [data.tile([P, UNIT_TILES, H], F32, name="rows%d" % j) for j in range(UNITS)]
+        noise_sb = data.tile([P, ROW_TILES, H], BF16, align_bytes=ALIGN)
+        rows_sb = [data.tile([P, UNIT_TILES, H], F32, name="rows%d" % j, align_bytes=ALIGN) for j in range(UNITS)]
         norms = const.tile([P, ROW_TILES], F32)
         x_codes = [
-            [data.tile([P, PASSES, MOVING], U32, name="x_codes%d_%d" % (c, n), align_bytes=64) for n in range(HALVES)]
+            [data.tile([P, PASSES, MOVING], U32, name="x_codes%d_%d" % (c, n), align_bytes=ALIGN) for n in range(HALVES)]
             for c in range(2)
         ]
         x_planes = [
-            [data.tile([P, PASSES, MOVING], U8, name="x_planes%d_%d" % (c, n), align_bytes=64) for n in range(HALVES)]
+            [data.tile([P, PASSES, MOVING], U8, name="x_planes%d_%d" % (c, n), align_bytes=ALIGN) for n in range(HALVES)]
             for c in range(2)
         ]
 
         zeros = const.tile([P, H], BF16)
         nc.gpsimd.memset(zeros[:].bitcast(F32), 0.0)
-        first_rows = const.tile([P, 2, H], BF16)
-        b2_row = const.tile([P, H], BF16)
+        first_rows = const.tile([P, 2, H], BF16, align_bytes=ALIGN)
+        b2_row = const.tile([P, H], BF16, align_bytes=ALIGN)
         b1_row, u_row = first_rows[:, 0, :], first_rows[:, 1, :]
         nc.vector.memset(first_rows[:].rearrange("p v h -> p (v h)").bitcast(I32), 0)
         table_warmer = const.tile([P, 1], F32)
@@ -79,11 +80,11 @@ def tile_splitnn_pa_kernel(
             nc.vector.memset(w_planes[c][:].bitcast(I32), 0)
         ones = const.tile([P, P], BF16)
         nc.vector.memset(ones[:], 1.0)
-        ident = const.tile([P, P], F32)
+        ident = const.tile([P, P], F32, align_bytes=ALIGN)
         make_identity(nc, ident[:])
 
         def load_x(c, first, end):
-            rows = data.tile([P, end - first, F], BF16, name="x%d_%d" % (c, first))
+            rows = data.tile([P, end - first, F], BF16, name="x%d_%d" % (c, first), align_bytes=ALIGN)
             nc.sync.dma_start(out=rows[:], in_=x_rows[c][:, first:end, :])
             for t in range(first, end):
                 x_sb[c][t] = rows[:, t - first, :]
@@ -113,8 +114,8 @@ def tile_splitnn_pa_kernel(
         nc.sync.dma_start(out=noise_sb[:], in_=noise_rows)
         nc.scalar.activation(out=table_warmer[:], in_=table_warmer[:], func=ACT.Abs)
 
-        b1_all = const.tile([P, H], F32)
-        keep_all = const.tile([P, H], F32)
+        b1_all = const.tile([P, H], F32, align_bytes=ALIGN)
+        keep_all = const.tile([P, H], F32, align_bytes=ALIGN)
         cols = const.tile([P, 2, H_SLICES], F32)
         b2_cols = cols[:, 0, :]
         keep_cols = const.tile([P, H_SLICES], F32)
@@ -156,7 +157,7 @@ def tile_splitnn_pa_kernel(
             j, i = divmod(t, UNIT_TILES)
             if (c, j) not in grouped:
                 grouped[c, j] = stage.tile(
-                    [P, PASSES, UNIT_TILES, P, PACK], BF16, align_bytes=64, tag="grouped", name="grouped"
+                    [P, PASSES, UNIT_TILES, P, PACK], BF16, align_bytes=ALIGN, tag="grouped", name="grouped"
                 )
             copy_out(
                 out=grouped[c, j][:, :, i, :, :].bitcast(F32),
@@ -280,7 +281,7 @@ def tile_splitnn_pa_kernel(
             out_ps = psum.tile([P, H_SLICES, P], F32, tag="bank")
             for a in range(H_SLICES):
                 nc.tensor.transpose(out_ps[:, a, :], out_cols[:, a, rows], ident[:])
-            out_sb = stage.tile([P, H], F32, tag="out_sb")
+            out_sb = stage.tile([P, H], F32, tag="out_sb", align_bytes=ALIGN)
             copy_out(out=out_sb[:], in_=out_ps[:].rearrange("p a m -> p (a m)"))
             nc.sync.dma_start(out=out_rows[:, t, :], in_=out_sb[:])
 
@@ -322,7 +323,7 @@ def tile_splitnn_pa_kernel(
             noisy_rows(t, multiplier)
         nc.vector.tensor_single_scalar(out=keep_cols[:], in_=cols[:, 1, :], scalar=P_KEEP, op=ALU.is_lt)
         d_cols_of = [
-            stage.tile([P, H_SLICES, MOVING], F32, tag="d_cols", name="d_cols", bufs=HALVES) for half in range(HALVES)
+            stage.tile([P, H_SLICES, MOVING], F32, tag="d_cols", name="d_cols", bufs=HALVES, align_bytes=ALIGN) for half in range(HALVES)
         ]
         client2_columns(0, d_cols_of[0], range(H_SLICES))
         for j in range(HALF_UNITS, UNITS):

@@ -274,7 +274,7 @@ def tile_splitnn_pa_kernel(
             for a in range(H_SLICES):
                 nc.tensor.transpose(d_rows[:, a, :], d_cols[:, a, rows], ident[:])
             nc.vector.tensor_tensor(out=c_rows, in0=c_rows, in1=d_rows[:].rearrange("p a m -> p (a m)"), op=ALU.min)
-            nc.sync.dma_start(out=out_rows[:, t, :], in_=c_rows)
+            nc.scalar.dma_start(out=out_rows[:, t, :], in_=c_rows)
 
         def store_rows(t, out_cols, copy_out):
             rows = slice((t % HALF_TILES) * P, (t % HALF_TILES + 1) * P)

from contextlib import ExitStack

import concourse.mybir as mybir
from concourse.masks import make_identity

F32 = mybir.dt.float32
BF16 = mybir.dt.bfloat16
I32 = mybir.dt.int32
U32 = mybir.dt.uint32
U8 = mybir.dt.uint8
FP8X4 = mybir.dt.float8_e4m3fn_x4
FP4X4 = mybir.dt.float4_e2m1fn_x4
ALU = mybir.AluOpType
ACT = mybir.ActivationFunctionType
AX = mybir.AxisListType

P = 128
B, F, H = 1024, 1024, 512
PACK = 4
K_PASS = P * PACK
PASSES = F // K_PASS
ROW_TILES = B // P
UNIT_TILES = 2
UNITS = ROW_TILES // UNIT_TILES
MOVING = 512
HALF_TILES = MOVING // P
HALF_UNITS = HALF_TILES // UNIT_TILES
HALVES = ROW_TILES // HALF_TILES
LAG = HALF_UNITS
H_SLICES = H // P
WORD_HALVES = 2
WARM_MATMULS = 3
ALIGN = 256
INV_EPS = 30.0 / 4.0
P_KEEP = 0.95

FLOPS = 2 * 2 * B * F * H


def tile_splitnn_pa_kernel(
    tc, x1, x2, W1_words, W1_scales, b1, W2_words, W2_scales, b2, noise_std, rr_uniform, out
):
    nc = tc.nc
    x_rows = [x.rearrange("(p t) k -> p t k", t=ROW_TILES) for x in (x1, x2)]
    noise_rows = noise_std.rearrange("(p t) h -> p t h", t=ROW_TILES)
    out_rows = out.rearrange("(p t) h -> p t h", t=ROW_TILES)

    with ExitStack() as ctx:
        const = ctx.enter_context(tc.tile_pool(name="const", bufs=1))
        data = ctx.enter_context(tc.tile_pool(name="data", bufs=1))
        stage = ctx.enter_context(tc.tile_pool(name="stage", bufs=UNITS))
        psum = ctx.enter_context(tc.psum_pool(name="psum", bufs=8))
        ctx.enter_context(tc.manual_schedule())

        w_words = [const.tile([P, PASSES, 2 * H], U8, name="w_words%d" % c, align_bytes=ALIGN) for c in range(2)]
        w_planes = [const.tile([P, PASSES, H], U8, name="w_planes%d" % c, align_bytes=ALIGN) for c in range(2)]
        x_sb = [{}, {}]
        noise_sb = data.tile([P, ROW_TILES, H], BF16, align_bytes=ALIGN)
        rows_sb = [data.tile([P, UNIT_TILES, H], F32, name="rows%d" % j, align_bytes=ALIGN) for j in range(UNITS)]
        norms = const.tile([P, ROW_TILES], F32)
        x_codes = [
            [data.tile([P, PASSES, MOVING], U32, name="x_codes%d_%d" % (c, n), align_bytes=ALIGN) for n in range(HALVES)]
            for c in range(2)
        ]
        x_planes = [
            [data.tile([P, PASSES, MOVING], U8, name="x_planes%d_%d" % (c, n), align_bytes=ALIGN) for n in range(HALVES)]
            for c in range(2)
        ]

        zeros = const.tile([P, H], BF16)
        nc.gpsimd.memset(zeros[:].bitcast(F32), 0.0)
        first_rows = const.tile([P, 2, H], BF16, align_bytes=ALIGN)
        b2_row = const.tile([P, H], BF16, align_bytes=ALIGN)
        b1_row, u_row = first_rows[:, 0, :], first_rows[:, 1, :]
        nc.vector.memset(first_rows[:].rearrange("p v h -> p (v h)").bitcast(I32), 0)
        table_warmer = const.tile([P, 1], F32)
        nc.vector.memset(table_warmer[:], 0.0)
        nc.vector.memset(b2_row[:].bitcast(I32), 0)
        for c in range(2):
            nc.vector.memset(w_planes[c][:].bitcast(I32), 0)
        ones = const.tile([P, P], BF16)
        nc.vector.memset(ones[:], 1.0)
        ident = const.tile([P, P], F32, align_bytes=ALIGN)
        make_identity(nc, ident[:])

        def load_x(c, first, end):
            rows = data.tile([P, end - first, F], BF16, name="x%d_%d" % (c, first), align_bytes=ALIGN)
            nc.sync.dma_start(out=rows[:], in_=x_rows[c][:, first:end, :])
            for t in range(first, end):
                x_sb[c][t] = rows[:, t - first, :]

        def load_weight(c, words, scales):
            nc.sync.dma_start(
                out=w_words[c][:].bitcast(I32), in_=words.bitcast(I32).rearrange("g p b -> p g b")
            )
            plane_words = w_planes[c][:].bitcast(I32)
            scale_rows = scales.bitcast(I32).rearrange("g (q l) n -> l q g n", l=4)
            for l in range(4):
                nc.sync.dma_start(out=plane_words[l:P:32, :, :], in_=scale_rows[l])

        load_x(0, 0, 1)
        load_x(0, 1, 2)
        nc.sync.dma_start(out=b1_row[0:1, :], in_=b1.unsqueeze(0))
        nc.sync.dma_start(out=u_row[0:1, :], in_=rr_uniform.unsqueeze(0))
        for first in range(UNIT_TILES, ROW_TILES, UNIT_TILES):
            if first == ROW_TILES - UNIT_TILES:
                load_weight(0, W1_words, W1_scales)
            load_x(0, first, first + UNIT_TILES)
        nc.sync.dma_start(out=b2_row[0:1, :], in_=b2.unsqueeze(0))
        for first in range(0, HALF_TILES, UNIT_TILES):
            load_x(1, first, first + UNIT_TILES)
        load_weight(1, W2_words, W2_scales)
        load_x(1, HALF_TILES, ROW_TILES)
        nc.sync.dma_start(out=noise_sb[:], in_=noise_rows)
        nc.scalar.activation(out=table_warmer[:], in_=table_warmer[:], func=ACT.Abs)

        b1_all = const.tile([P, H], F32, align_bytes=ALIGN)
        keep_all = const.tile([P, H], F32, align_bytes=ALIGN)
        cols = const.tile([P, 2, H_SLICES], F32)
        b2_cols = cols[:, 0, :]
        keep_cols = const.tile([P, H_SLICES], F32)

        def spread_vectors():
            spread_ps = psum.tile([P, H], F32, tag="bank")
            nc.tensor.matmul(out=spread_ps[:], lhsT=ones[:], rhs=b1_row, start=True, stop=True)
            nc.scalar.copy(out=b1_all[:], in_=spread_ps[:])
            u_ps = psum.tile([P, H], F32, tag="bank")
            nc.tensor.matmul(out=u_ps[:], lhsT=ones[:], rhs=u_row, start=True, stop=True)
            nc.vector.tensor_single_scalar(out=keep_all[:], in_=u_ps[:], scalar=P_KEEP, op=ALU.is_lt)

        def column_vectors():
            cols_ps = psum.tile([P, 2, H_SLICES], F32, tag="bank")
            for v, row in enumerate((b2_row, u_row)):
                for a in range(H_SLICES):
                    nc.tensor.matmul(
                        out=cols_ps[:, v, a : a + 1], lhsT=row[:, a * P : (a + 1) * P],
                        rhs=ones[:, 0:1], start=True, stop=True,
                    )
            nc.scalar.copy(out=cols[:], in_=cols_ps[:])

        turned, grouped = {}, {}
        extremes = (ALU.max, ALU.min)

        def transpose_tile(c, t):
            x_words = x_sb[c][t].bitcast(F32)
            turned[c, t] = psum.tile([P, PASSES * WORD_HALVES, P], F32, tag="bank", name="turned")
            for g in range(PASSES):
                first = g * K_PASS // 2
                for u in range(WORD_HALVES):
                    nc.tensor.transpose(
                        turned[c, t][:, g * WORD_HALVES + u, :],
                        x_words[:, first + u : first + K_PASS // 2 : WORD_HALVES],
                        ident[:],
                    )

        def group_tile(c, t, copy_out):
            j, i = divmod(t, UNIT_TILES)
            if (c, j) not in grouped:
                grouped[c, j] = stage.tile(
                    [P, PASSES, UNIT_TILES, P, PACK], BF16, align_bytes=ALIGN, tag="grouped", name="grouped"
                )
            copy_out(
                out=grouped[c, j][:, :, i, :, :].bitcast(F32),
                in_=turned[c, t][:].rearrange("p (g u) r -> p g r u", u=WORD_HALVES),
            )

        def transpose_unit(c, j, copies):
            for i in range(UNIT_TILES):
                transpose_tile(c, j * UNIT_TILES + i)
                group_tile(c, j * UNIT_TILES + i, copies[i])

        def quantise_unit(c, j):
            half = j // HALF_UNITS
            rows = slice((j % HALF_UNITS) * UNIT_TILES * P, (j % HALF_UNITS + 1) * UNIT_TILES * P)
            for g in range(PASSES):
                nc.vector.quantize_mx(
                    out=x_codes[c][half][:, g, rows].bitcast(FP8X4),
                    scales=x_planes[c][half][:, g, rows],
                    in_=grouped[c, j][:, g, :, :, :].rearrange("p i r s -> p (i r s)"),
                )

        def client1_rows(j):
            half = j // HALF_UNITS
            for i in range(UNIT_TILES):
                t = j * UNIT_TILES + i
                rows = slice((t % HALF_TILES) * P, (t % HALF_TILES + 1) * P)
                acc = psum.tile([P, H], F32, tag="bank")
                for g in range(PASSES):
                    nc.tensor.matmul_mx(
                        out=acc[:],
                        lhsT=x_codes[0][half][:, g, rows].bitcast(FP8X4),
                        lhsT_scale=x_planes[0][half][:, g, rows],
                        rhs=w_words[0][:, g, :].bitcast(FP4X4),
                        rhs_scale=w_planes[0][:, g, :],
                        start=(g == 0),
                        stop=(g == PASSES - 1),
                    )
                nc.vector.tensor_tensor(out=rows_sb[j][:, i, :], in0=acc[:], in1=b1_all[:], op=ALU.add)

        def row_norms(t):
            absolute = stage.tile([P, H], BF16, tag="absolute")
            nc.scalar.activation(
                out=absolute[:], in_=rows_sb[t // UNIT_TILES][:, t % UNIT_TILES, :], func=ACT.Abs,
                accum_out=norms[:, t : t + 1],
            )

        def extremes_across():
            part = const.tile([P, 2], F32)
            for e, extreme in enumerate(extremes):
                nc.vector.tensor_reduce(out=part[:, e : e + 1], in_=norms[:], axis=AX.X, op=extreme)
            across = psum.tile([P, 2, P], F32, tag="bank")
            for e in range(2):
                nc.tensor.transpose(across[:, e, :], part[:, e : e + 1].to_broadcast([P, P]), ident[:])
            return across

        def noise_multiplier(across):
            both = const.tile([P, 2], F32)
            for e, extreme in enumerate(extremes):
                nc.vector.tensor_reduce(out=both[:, e : e + 1], in_=across[:, e, :], axis=AX.X, op=extreme)
            multiplier = const.tile([P, 1], F32)
            nc.vector.tensor_scalar(
                out=multiplier[:], in0=both[:, 0:1], scalar1=both[:, 1:2], scalar2=INV_EPS,
                op0=ALU.subtract, op1=ALU.mult,
            )
            return multiplier

        def client2_columns(half, d_cols, slices):
            for a in slices:
                acc = psum.tile([P, MOVING], F32, tag="bank")
                for g in range(PASSES):
                    nc.tensor.matmul_mx(
                        out=acc[:],
                        lhsT=w_words[1][:, g, 2 * P * a : 2 * P * (a + 1)].bitcast(FP4X4),
                        lhsT_scale=w_planes[1][:, g, P * a : P * (a + 1)],
                        rhs=x_codes[1][half][:, g, :].bitcast(FP8X4),
                        rhs_scale=x_planes[1][half][:, g, :],
                        start=(g == 0),
                        stop=(g == PASSES - 1),
                    )
                nc.scalar.activation(
                    out=d_cols[:, a, :], in_=acc[:], func=ACT.Identity, bias=b2_cols[:, a : a + 1]
                )

        def noisy_rows(t, multiplier):
            rows = rows_sb[t // UNIT_TILES][:, t % UNIT_TILES, :]
            nc.vector.scalar_tensor_tensor(
                out=rows, in0=noise_sb[:, t, :], scalar=multiplier[:, 0:1], in1=rows, op0=ALU.mult, op1=ALU.add
            )

        def fuse_columns(j, d_cols):
            first = (j % HALF_UNITS) * UNIT_TILES
            rows = slice(first * P, (first + UNIT_TILES) * P)
            for pair in range(H_SLICES // 2):
                c_cols = psum.tile([P, 2, UNIT_TILES, P], F32, tag="bank")
                for s in range(2):
                    a = 2 * pair + s
                    for i in range(UNIT_TILES):
                        nc.tensor.transpose(c_cols[:, s, i, :], rows_sb[j][:, i, a * P : (a + 1) * P], ident[:])
                for s in range(2):
                    a = 2 * pair + s
                    nc.vector.scalar_tensor_tensor(
                        out=d_cols[:, a, rows], in0=c_cols[:, s, :, :].rearrange("p i r -> p (i r)"),
                        scalar=keep_cols[:, a : a + 1], in1=d_cols[:, a, rows], op0=ALU.mult, op1=ALU.min,
                    )

        def mask_rows(t, engine):
            rows = rows_sb[t // UNIT_TILES][:, t % UNIT_TILES, :]
            engine.tensor_tensor(out=rows, in0=rows, in1=keep_all[:], op=ALU.mult)

        def finish_rows(t, d_cols):
            rows = slice((t % HALF_TILES) * P, (t % HALF_TILES + 1) * P)
            c_rows = rows_sb[t // UNIT_TILES][:, t % UNIT_TILES, :]
            d_rows = psum.tile([P, H_SLICES, P], F32, tag="bank")
            for a in range(H_SLICES):
                nc.tensor.transpose(d_rows[:, a, :], d_cols[:, a, rows], ident[:])
            nc.vector.tensor_tensor(out=c_rows, in0=c_rows, in1=d_rows[:].rearrange("p a m -> p (a m)"), op=ALU.min)
            nc.scalar.dma_start(out=out_rows[:, t, :], in_=c_rows)

        def store_rows(t, out_cols, copy_out):
            rows = slice((t % HALF_TILES) * P, (t % HALF_TILES + 1) * P)
            out_ps = psum.tile([P, H_SLICES, P], F32, tag="bank")
            for a in range(H_SLICES):
                nc.tensor.transpose(out_ps[:, a, :], out_cols[:, a, rows], ident[:])
            out_sb = stage.tile([P, H], F32, tag="out_sb", align_bytes=ALIGN)
            copy_out(out=out_sb[:], in_=out_ps[:].rearrange("p a m -> p (a m)"))
            nc.sync.dma_start(out=out_rows[:, t, :], in_=out_sb[:])

        warm_ps = psum.tile([P, H], F32, tag="bank")
        for n in range(WARM_MATMULS):
            nc.tensor.matmul(out=warm_ps[:], lhsT=zeros[:, :P], rhs=zeros[:], start=True, stop=True)
        by_scalar = [nc.scalar.copy] * UNIT_TILES
        shared = [nc.scalar.copy, nc.vector.tensor_copy]
        transpose_unit(0, 0, shared)
        quantise_unit(0, 0)
        spread_vectors()
        transpose_unit(0, 1, by_scalar)
        quantise_unit(0, 1)
        transpose_unit(0, 2, by_scalar)
        client1_rows(0)
        quantise_unit(0, 2)
        row_norms(0)
        transpose_unit(0, 3, by_scalar)
        row_norms(1)
        for j in range(1, UNITS):
            client1_rows(j)
            if j == 1:
                quantise_unit(0, UNITS - 1)
            for t in range(j * UNIT_TILES, (j + 1) * UNIT_TILES):
                row_norms(t)

        column_vectors()
        for t in range(HALF_TILES):
            transpose_tile(1, t)
        for t in range(HALF_TILES):
            group_tile(1, t, nc.vector.tensor_copy if t < UNIT_TILES else nc.scalar.copy)
        across = extremes_across()
        quantise_unit(1, 0)
        multiplier = noise_multiplier(across)
        quantise_unit(1, 1)
        for j in range(HALF_UNITS, UNITS):
            transpose_unit(1, j, by_scalar)
        for t in range(HALF_TILES):
            noisy_rows(t, multiplier)
        nc.vector.tensor_single_scalar(out=keep_cols[:], in_=cols[:, 1, :], scalar=P_KEEP, op=ALU.is_lt)
        d_cols_of = [
            stage.tile([P, H_SLICES, MOVING], F32, tag="d_cols", name="d_cols", bufs=HALVES, align_bytes=ALIGN) for half in range(HALVES)
        ]
        client2_columns(0, d_cols_of[0], range(H_SLICES))
        for j in range(HALF_UNITS, UNITS):
            quantise_unit(1, j)
        noisy_rows(ROW_TILES - 1, multiplier)
        mask_rows(ROW_TILES - 1, nc.gpsimd)
        for j in range(HALF_UNITS):
            fuse_columns(j, d_cols_of[0])
        slices = range(H_SLICES)
        for j in range(HALF_UNITS):
            client2_columns(1, d_cols_of[1], slices[j * H_SLICES // HALF_UNITS : (j + 1) * H_SLICES // HALF_UNITS])
            for t in range(j * UNIT_TILES, (j + 1) * UNIT_TILES):
                store_rows(t, d_cols_of[0], nc.scalar.copy)
        for t in range(HALF_TILES, ROW_TILES - 1):
            noisy_rows(t, multiplier)
        for t in range(HALF_TILES, ROW_TILES - 1):
            mask_rows(t, nc.vector)
        for t in range(HALF_TILES, ROW_TILES):
            finish_rows(t, d_cols_of[1])
